import numpy as np
import ml_dtypes


def mxq(x, axis, fmt="e4m3"):
    dtype, down = {"e4m3": (ml_dtypes.float8_e4m3fn, 7), "e5m2": (ml_dtypes.float8_e5m2, 14)}[fmt]
    v = np.moveaxis(np.asarray(x, np.float32).astype(ml_dtypes.bfloat16).astype(np.float64), axis, -1)
    blocks = v.reshape(v.shape[:-1] + (-1, 32))
    amax = np.abs(blocks).max(-1, keepdims=True)
    byte = np.maximum(np.where(amax > 0, np.frexp(amax)[1] - 1 + 127, 0) - down, 1)
    scale = np.exp2(byte - 127.0)
    codes = (blocks / scale).astype(np.float32).astype(dtype).astype(np.float64)
    return np.moveaxis((codes * scale).reshape(v.shape), -1, axis)


WIDE = False


def mx_kscale(k):
    if not WIDE:
        return np.ones(k)
    levels = np.array([10, -10, 5, -5, 0])
    a = np.random.permutation(np.resize(levels, k // 512 * 4)).reshape(k // 512, 4)
    idx = np.arange(k)
    return np.exp2(a[idx // 512, idx % 128 // 32])


BF16 = ml_dtypes.bfloat16


def bf(x):
    return np.asarray(x, np.float32).astype(BF16)


def f64(x):
    return np.asarray(x).astype(np.float64)


N, MI0, MI1, MS, MG, MO0, MO1, DV = 256, 1024, 512, 2048, 1024, 1024, 512, 3


def silu(v):
    return v / (1.0 + np.exp(-v))


def sigmoid(v):
    return 1.0 / (1.0 + np.exp(-v))


def irlin(x, mul0, mul1, w0, w1):
    n = x.shape[0]
    x0 = x[:, :mul0]
    x1 = x[:, mul0:].reshape(n, mul1, DV).transpose(0, 2, 1)
    y0 = (mxq(x0, 1, "e4m3") @ mxq(w0, 0, "e4m3")) * (1.0 / np.sqrt(mul0))
    y1 = (mxq(x1, 2, "e4m3") @ mxq(w1, 0, "e4m3")).transpose(0, 2, 1) * (1.0 / np.sqrt(mul1))
    return np.concatenate([y0, y1.reshape(n, -1)], axis=-1)


def gate(h):
    n = h.shape[0]
    s = silu(h[:, :MS])
    g = sigmoid(h[:, MS:MS + MG])
    v = h[:, MS + MG:].reshape(n, MG, DV)
    return np.concatenate([s, (v * g[:, :, None]).reshape(n, -1)], axis=-1)


def setup_inputs():
    s0, s1, t = mx_kscale(MI0), mx_kscale(MI1), mx_kscale(MG)
    x0 = np.random.standard_normal((N, MI0)) * s0
    x1 = np.random.standard_normal((N, MI1, DV)) * s1[None, :, None]
    return {"features": bf(np.concatenate([x0, x1.reshape(N, -1)], axis=-1)),
            "lin1_W0": bf(np.random.standard_normal((MI0, MS + MG)) / s0[:, None]),
            "lin1_W1": bf(np.random.standard_normal((MI1, MG)) / s1[:, None] * t[None, :]),
            "lin2_W0": bf(np.random.standard_normal((MS, MS + MG))),
            "lin2_W1": bf(np.random.standard_normal((MG, MG)) / t[:, None])}


def reference(features, lin1_W0, lin1_W1, lin2_W0, lin2_W1):
    h = irlin(f64(features), MI0, MI1, f64(lin1_W0), f64(lin1_W1))
    h = gate(h)
    h = irlin(h, MS, MG, f64(lin2_W0), f64(lin2_W1))
    return gate(h)

@@ -1,0 +1,300 @@
+import math
+
+import concourse.mybir as mybir
+from concourse.masks import make_identity
+
+BF16 = mybir.dt.bfloat16
+F32 = mybir.dt.float32
+U32 = mybir.dt.uint32
+U8 = mybir.dt.uint8
+FP8X4 = mybir.dt.float8_e4m3fn_x4
+ACT = mybir.ActivationFunctionType
+ALU = mybir.AluOpType
+
+P = 128
+PACK = 4
+K_PASS = P * PACK
+BANK = 512
+
+NODES = 256
+NODE_TILES = NODES // P
+DV = 3
+IN_S = 1024
+IN_V = 512
+HID_S = 2048
+HID_V = 1024
+LIN_S = HID_S + HID_V
+
+CHUNK = 1024
+RUN = 4
+VECTOR_COLS = 512
+
+FLOPS = 2 * NODES * (IN_S + HID_S) * LIN_S + 2 * NODES * DV * (IN_V + HID_V) * HID_V
+
+
+def tile_feedforward_pa_kernel(tc, features, lin1_W0, lin1_W1, lin2_W0, lin2_W1, out):
+    nc = tc.nc
+
+    with tc.tile_pool(name="keep", bufs=1) as keep, tc.tile_pool(
+        name="stream", bufs=1
+    ) as stream, tc.psum_pool(name="psum_s", bufs=4) as psum_s, tc.psum_pool(
+        name="psum_v", bufs=4
+    ) as psum_v:
+
+        def quantise_weight_chunk(w, g, col0, codes, scales):
+            cols = slice(col0, col0 + CHUNK)
+            raw = stream.tile([P, PACK, CHUNK], BF16, bufs=4)
+            nc.sync.dma_start(
+                out=raw[:],
+                in_=w[g * K_PASS : (g + 1) * K_PASS, cols].rearrange("(t p) w -> p t w", p=P),
+            )
+            grouped = stream.tile([P, CHUNK, PACK], BF16, bufs=3, align_bytes=64)
+            src = raw[:].rearrange("p t (c i) -> p c t i", i=RUN)
+            dst = grouped[:].rearrange("p (c i) t -> p c t i", i=RUN)
+            split = VECTOR_COLS // RUN
+            nc.vector.tensor_copy(out=dst[:, :split], in_=src[:, :split])
+            nc.scalar.copy(out=dst[:, split:], in_=src[:, split:])
+            nc.vector.quantize_mx(
+                out=codes[:, g, cols].bitcast(FP8X4),
+                scales=scales[:, g, cols],
+                in_=grouped[:].rearrange("p w t -> p (w t)"),
+            )
+
+        def mx(acc, a_codes, a_scales, b_codes, b_scales, start, stop):
+            nc.tensor.matmul_mx(
+                out=acc,
+                lhsT=a_codes.bitcast(FP8X4),
+                lhsT_scale=a_scales,
+                rhs=b_codes.bitcast(FP8X4),
+                rhs_scale=b_scales,
+                start=start,
+                stop=stop,
+            )
+
+        s_passes = HID_S // K_PASS
+        v_passes = HID_V // K_PASS
+        w20_codes = keep.tile([P, s_passes, LIN_S], U32, align_bytes=64)
+        w20_scales = keep.tile([P, s_passes, LIN_S], U8, align_bytes=64)
+        w21_codes = keep.tile([P, v_passes, HID_V], U32, align_bytes=64)
+        w21_scales = keep.tile([P, v_passes, HID_V], U8, align_bytes=64)
+        g1s_codes = keep.tile([P, s_passes, NODES], U32, align_bytes=64)
+        g1s_scales = keep.tile([P, s_passes, NODES], U8, align_bytes=64)
+        g1v_codes = keep.tile([P, v_passes, DV, NODES], U32, align_bytes=64)
+        g1v_scales = keep.tile([P, v_passes, DV, NODES], U8, align_bytes=64)
+        gate2 = keep.tile([P, NODE_TILES, HID_V], F32)
+
+        with tc.tile_pool(name="layer1", bufs=1) as layer1:
+            in_passes = IN_S // K_PASS
+            ident = layer1.tile([P, P], BF16)
+            make_identity(nc, ident[:])
+
+            x_sb = []
+            for nt in range(NODE_TILES):
+                x_rows = layer1.tile([P, IN_S + DV * IN_V], BF16, name="x_rows%d" % nt)
+                nc.sync.dma_start(out=x_rows[:], in_=features[nt * P : (nt + 1) * P, :])
+                x_sb.append(x_rows)
+
+            xs_grouped = layer1.tile([P, in_passes, NODES, PACK], BF16, align_bytes=64)
+            xv_grouped = layer1.tile([P, DV, NODES, PACK], BF16, align_bytes=64)
+            xs_codes = layer1.tile([P, in_passes, NODES], U32, align_bytes=64)
+            xs_scales = layer1.tile([P, in_passes, NODES], U8, align_bytes=64)
+            xv_codes = layer1.tile([P, DV, NODES], U32, align_bytes=64)
+            xv_scales = layer1.tile([P, DV, NODES], U8, align_bytes=64)
+            for nt in range(NODE_TILES):
+                nodes = slice(nt * P, (nt + 1) * P)
+                for g in range(in_passes):
+                    flipped = psum_s.tile([P, PACK, P], BF16, tag="bank")
+                    for t in range(PACK):
+                        k0 = g * K_PASS + t * P
+                        nc.tensor.transpose(flipped[:, t, :], x_sb[nt][:, k0 : k0 + P], ident[:])
+                    nc.scalar.copy(
+                        out=xs_grouped[:, g, nodes, :], in_=flipped[:].rearrange("p t n -> p n t")
+                    )
+                x_vec = x_sb[nt][:, IN_S:].rearrange("n (i d) -> n d i", d=DV)
+                for d in range(DV):
+                    flipped = psum_v.tile([P, PACK, P], BF16, tag="bank")
+                    for t in range(PACK):
+                        nc.tensor.transpose(
+                            flipped[:, t, :], x_vec[:, d, t * P : (t + 1) * P], ident[:]
+                        )
+                    nc.vector.tensor_copy(
+                        out=xv_grouped[:, d, nodes, :], in_=flipped[:].rearrange("p t n -> p n t")
+                    )
+            nc.vector.quantize_mx(
+                out=xs_codes[:].rearrange("p g n -> p (g n)").bitcast(FP8X4),
+                scales=xs_scales[:].rearrange("p g n -> p (g n)"),
+                in_=xs_grouped[:].rearrange("p g n t -> p (g n t)"),
+            )
+            for d in range(DV):
+                nc.vector.quantize_mx(
+                    out=xv_codes[:, d, :].bitcast(FP8X4),
+                    scales=xv_scales[:, d, :],
+                    in_=xv_grouped[:, d, :, :].rearrange("p n t -> p (n t)"),
+                )
+
+            w10_codes = layer1.tile([P, in_passes, LIN_S], U32, align_bytes=64)
+            w10_scales = layer1.tile([P, in_passes, LIN_S], U8, align_bytes=64)
+            w11_codes = layer1.tile([P, 1, HID_V], U32, align_bytes=64)
+            w11_scales = layer1.tile([P, 1, HID_V], U8, align_bytes=64)
+            gate1 = layer1.tile([P, v_passes, NODES, PACK], F32)
+
+            def layer1_scalars(channel0, nt):
+                nodes = slice(nt * P, (nt + 1) * P)
+                bank = psum_s.tile([P, PACK, P], F32, tag="bank")
+                for t in range(PACK):
+                    chans = slice(channel0 + t * P, channel0 + (t + 1) * P)
+                    for g in range(in_passes):
+                        mx(
+                            bank[:, t, :],
+                            w10_codes[:, g, chans],
+                            w10_scales[:, g, chans],
+                            xs_codes[:, g, nodes],
+                            xs_scales[:, g, nodes],
+                            start=(g == 0),
+                            stop=(g == in_passes - 1),
+                        )
+                return bank
+
+            for col0 in range(0, HID_S, CHUNK):
+                for g in range(in_passes):
+                    quantise_weight_chunk(lin1_W0, g, col0, w10_codes, w10_scales)
+                for h in range(col0 // K_PASS, (col0 + CHUNK) // K_PASS):
+                    s_grouped = layer1.tile([P, NODES, PACK], BF16, bufs=3, align_bytes=64)
+                    for nt in range(NODE_TILES):
+                        bank = layer1_scalars(h * K_PASS, nt)
+                        nc.scalar.activation(
+                            out=s_grouped[:, nt * P : (nt + 1) * P, :],
+                            in_=bank[:].rearrange("p t n -> p n t"),
+                            func=ACT.Silu,
+                            scale=1.0 / math.sqrt(IN_S),
+                        )
+                    nc.vector.quantize_mx(
+                        out=g1s_codes[:, h, :].bitcast(FP8X4),
+                        scales=g1s_scales[:, h, :],
+                        in_=s_grouped[:].rearrange("p n t -> p (n t)"),
+                    )
+
+            for g in range(in_passes):
+                quantise_weight_chunk(lin1_W0, g, HID_S, w10_codes, w10_scales)
+            for h in range(v_passes):
+                for nt in range(NODE_TILES):
+                    bank = layer1_scalars(HID_S + h * K_PASS, nt)
+                    nc.scalar.activation(
+                        out=gate1[:, h, nt * P : (nt + 1) * P, :],
+                        in_=bank[:].rearrange("p t n -> p n t"),
+                        func=ACT.Sigmoid,
+                        scale=1.0 / math.sqrt(IN_S),
+                    )
+
+            quantise_weight_chunk(lin1_W1, 0, 0, w11_codes, w11_scales)
+            for h in range(v_passes):
+                for d in range(DV):
+                    v_grouped = layer1.tile([P, NODES, PACK], BF16, bufs=3, align_bytes=64)
+                    for nt in range(NODE_TILES):
+                        nodes = slice(nt * P, (nt + 1) * P)
+                        bank = psum_v.tile([P, PACK, P], F32, tag="bank")
+                        for t in range(PACK):
+                            chans = slice(h * K_PASS + t * P, h * K_PASS + (t + 1) * P)
+                            mx(
+                                bank[:, t, :],
+                                w11_codes[:, 0, chans],
+                                w11_scales[:, 0, chans],
+                                xv_codes[:, d, nodes],
+                                xv_scales[:, d, nodes],
+                                start=True,
+                                stop=True,
+                            )
+                        nc.vector.scalar_tensor_tensor(
+                            out=v_grouped[:, nodes, :],
+                            in0=bank[:].rearrange("p t n -> p n t"),
+                            scalar=1.0 / math.sqrt(IN_V),
+                            in1=gate1[:, h, nodes, :],
+                            op0=ALU.mult,
+                            op1=ALU.mult,
+                        )
+                    nc.vector.quantize_mx(
+                        out=g1v_codes[:, h, d, :].bitcast(FP8X4),
+                        scales=g1v_scales[:, h, d, :],
+                        in_=v_grouped[:].rearrange("p n t -> p (n t)"),
+                    )
+
+        def layer2_scalars(col0):
+            banks = [
+                [psum_s.tile([P, BANK], F32, name="acc", tag="bank") for j in range(CHUNK // BANK)]
+                for nt in range(NODE_TILES)
+            ]
+            for h in range(s_passes):
+                quantise_weight_chunk(lin2_W0, h, col0, w20_codes, w20_scales)
+                for nt in range(NODE_TILES):
+                    nodes = slice(nt * P, (nt + 1) * P)
+                    for j in range(CHUNK // BANK):
+                        cols = slice(col0 + j * BANK, col0 + (j + 1) * BANK)
+                        mx(
+                            banks[nt][j][:],
+                            g1s_codes[:, h, nodes],
+                            g1s_scales[:, h, nodes],
+                            w20_codes[:, h, cols],
+                            w20_scales[:, h, cols],
+                            start=(h == 0),
+                            stop=(h == s_passes - 1),
+                        )
+            return banks
+
+        banks = layer2_scalars(HID_S)
+        for nt in range(NODE_TILES):
+            for j in range(CHUNK // BANK):
+                nc.scalar.activation(
+                    out=gate2[:, nt, j * BANK : (j + 1) * BANK],
+                    in_=banks[nt][j][:],
+                    func=ACT.Sigmoid,
+                    scale=1.0 / math.sqrt(HID_S),
+                )
+
+        with tc.tile_pool(name="layer2", bufs=3) as layer2:
+            for h in range(v_passes):
+                quantise_weight_chunk(lin2_W1, h, 0, w21_codes, w21_scales)
+            for nt in range(NODE_TILES):
+                nodes = slice(nt * P, (nt + 1) * P)
+                for c0 in range(0, HID_V, BANK):
+                    v_out = layer2.tile([P, BANK, DV], F32)
+                    for c1 in range(0, BANK, P):
+                        chans = slice(c0 + c1, c0 + c1 + P)
+                        bank = psum_v.tile([P, DV, P], F32, tag="bank")
+                        for d in range(DV):
+                            for h in range(v_passes):
+                                mx(
+                                    bank[:, d, :],
+                                    g1v_codes[:, h, d, nodes],
+                                    g1v_scales[:, h, d, nodes],
+                                    w21_codes[:, h, chans],
+                                    w21_scales[:, h, chans],
+                                    start=(h == 0),
+                                    stop=(h == v_passes - 1),
+                                )
+                        nc.vector.scalar_tensor_tensor(
+                            out=v_out[:, c1 : c1 + P, :],
+                            in0=bank[:].rearrange("p d o -> p o d"),
+                            scalar=1.0 / math.sqrt(HID_V),
+                            in1=gate2[:, nt, chans].unsqueeze(2).to_broadcast([P, P, DV]),
+                            op0=ALU.mult,
+                            op1=ALU.mult,
+                        )
+                    nc.sync.dma_start(
+                        out=out[nodes, HID_S + DV * c0 : HID_S + DV * (c0 + BANK)],
+                        in_=v_out[:].rearrange("p o d -> p (o d)"),
+                    )
+
+            for col0 in range(0, HID_S, CHUNK):
+                banks = layer2_scalars(col0)
+                for nt in range(NODE_TILES):
+                    s_out = layer2.tile([P, CHUNK], F32)
+                    for j in range(CHUNK // BANK):
+                        nc.scalar.activation(
+                            out=s_out[:, j * BANK : (j + 1) * BANK],
+                            in_=banks[nt][j][:],
+                            func=ACT.Silu,
+                            scale=1.0 / math.sqrt(HID_S),
+                        )
+                    nc.sync.dma_start(
+                        out=out[nt * P : (nt + 1) * P, col0 : col0 + CHUNK], in_=s_out[:]
+                    )

@@ -26,14 +26,19 @@ HID_V = 1024
 LIN_S = HID_S + HID_V
 
 CHUNK = 1024
+HALF = CHUNK // 2
 RUN = 4
-VECTOR_COLS = 512
+V_STORE = 512
+RAW_BUFS = 6
 
 FLOPS = 2 * NODES * (IN_S + HID_S) * LIN_S + 2 * NODES * DV * (IN_V + HID_V) * HID_V
 
 
 def tile_feedforward_pa_kernel(tc, features, lin1_W0, lin1_W1, lin2_W0, lin2_W1, out):
     nc = tc.nc
+    in_passes = IN_S // K_PASS
+    s_passes = HID_S // K_PASS
+    v_passes = HID_V // K_PASS
 
     with tc.tile_pool(name="keep", bufs=1) as keep, tc.tile_pool(
         name="stream", bufs=1
@@ -42,23 +47,29 @@ def tile_feedforward_pa_kernel(tc, features, lin1_W0, lin1_W1, lin2_W0, lin2_W1,
     ) as psum_v:
 
         def quantise_weight_chunk(w, g, col0, codes, scales):
-            cols = slice(col0, col0 + CHUNK)
-            raw = stream.tile([P, PACK, CHUNK], BF16, bufs=4)
+            raw = stream.tile([P, PACK, CHUNK], BF16, bufs=RAW_BUFS)
             nc.sync.dma_start(
                 out=raw[:],
-                in_=w[g * K_PASS : (g + 1) * K_PASS, cols].rearrange("(t p) w -> p t w", p=P),
+                in_=w[g * K_PASS : (g + 1) * K_PASS, col0 : col0 + CHUNK].rearrange(
+                    "(t p) w -> p t w", p=P
+                ),
             )
-            grouped = stream.tile([P, CHUNK, PACK], BF16, bufs=3, align_bytes=64)
-            src = raw[:].rearrange("p t (c i) -> p c t i", i=RUN)
-            dst = grouped[:].rearrange("p (c i) t -> p c t i", i=RUN)
-            split = VECTOR_COLS // RUN
-            nc.vector.tensor_copy(out=dst[:, :split], in_=src[:, :split])
-            nc.scalar.copy(out=dst[:, split:], in_=src[:, split:])
-            nc.vector.quantize_mx(
-                out=codes[:, g, cols].bitcast(FP8X4),
-                scales=scales[:, g, cols],
-                in_=grouped[:].rearrange("p w t -> p (w t)"),
-            )
+            for half, copy in enumerate((nc.vector.tensor_copy, nc.scalar.copy)):
+                grouped = stream.tile(
+                    [P, HALF, PACK], BF16, name="grouped%d" % half, bufs=3, align_bytes=64
+                )
+                copy(
+                    out=grouped[:].rearrange("p (c i) t -> p c t i", i=RUN),
+                    in_=raw[:, :, half * HALF : (half + 1) * HALF].rearrange(
+                        "p t (c i) -> p c t i", i=RUN
+                    ),
+                )
+                cols = slice(col0 + half * HALF, col0 + (half + 1) * HALF)
+                nc.vector.quantize_mx(
+                    out=codes[:, g, cols].bitcast(FP8X4),
+                    scales=scales[:, g, cols],
+                    in_=grouped[:].rearrange("p w t -> p (w t)"),
+                )
 
         def mx(acc, a_codes, a_scales, b_codes, b_scales, start, stop):
             nc.tensor.matmul_mx(
@@ -71,8 +82,6 @@ def tile_feedforward_pa_kernel(tc, features, lin1_W0, lin1_W1, lin2_W0, lin2_W1,
                 stop=stop,
             )
 
-        s_passes = HID_S // K_PASS
-        v_passes = HID_V // K_PASS
         w20_codes = keep.tile([P, s_passes, LIN_S], U32, align_bytes=64)
         w20_scales = keep.tile([P, s_passes, LIN_S], U8, align_bytes=64)
         w21_codes = keep.tile([P, v_passes, HID_V], U32, align_bytes=64)
@@ -84,59 +93,61 @@ def tile_feedforward_pa_kernel(tc, features, lin1_W0, lin1_W1, lin2_W0, lin2_W1,
         gate2 = keep.tile([P, NODE_TILES, HID_V], F32)
 
         with tc.tile_pool(name="layer1", bufs=1) as layer1:
-            in_passes = IN_S // K_PASS
-            ident = layer1.tile([P, P], BF16)
-            make_identity(nc, ident[:])
-
-            x_sb = []
-            for nt in range(NODE_TILES):
-                x_rows = layer1.tile([P, IN_S + DV * IN_V], BF16, name="x_rows%d" % nt)
-                nc.sync.dma_start(out=x_rows[:], in_=features[nt * P : (nt + 1) * P, :])
-                x_sb.append(x_rows)
-
-            xs_grouped = layer1.tile([P, in_passes, NODES, PACK], BF16, align_bytes=64)
-            xv_grouped = layer1.tile([P, DV, NODES, PACK], BF16, align_bytes=64)
-            xs_codes = layer1.tile([P, in_passes, NODES], U32, align_bytes=64)
-            xs_scales = layer1.tile([P, in_passes, NODES], U8, align_bytes=64)
-            xv_codes = layer1.tile([P, DV, NODES], U32, align_bytes=64)
-            xv_scales = layer1.tile([P, DV, NODES], U8, align_bytes=64)
-            for nt in range(NODE_TILES):
-                nodes = slice(nt * P, (nt + 1) * P)
-                for g in range(in_passes):
-                    flipped = psum_s.tile([P, PACK, P], BF16, tag="bank")
-                    for t in range(PACK):
-                        k0 = g * K_PASS + t * P
-                        nc.tensor.transpose(flipped[:, t, :], x_sb[nt][:, k0 : k0 + P], ident[:])
-                    nc.scalar.copy(
-                        out=xs_grouped[:, g, nodes, :], in_=flipped[:].rearrange("p t n -> p n t")
-                    )
-                x_vec = x_sb[nt][:, IN_S:].rearrange("n (i d) -> n d i", d=DV)
-                for d in range(DV):
-                    flipped = psum_v.tile([P, PACK, P], BF16, tag="bank")
-                    for t in range(PACK):
-                        nc.tensor.transpose(
-                            flipped[:, t, :], x_vec[:, d, t * P : (t + 1) * P], ident[:]
-                        )
-                    nc.vector.tensor_copy(
-                        out=xv_grouped[:, d, nodes, :], in_=flipped[:].rearrange("p t n -> p n t")
-                    )
-            nc.vector.quantize_mx(
-                out=xs_codes[:].rearrange("p g n -> p (g n)").bitcast(FP8X4),
-                scales=xs_scales[:].rearrange("p g n -> p (g n)"),
-                in_=xs_grouped[:].rearrange("p g n t -> p (g n t)"),
-            )
-            for d in range(DV):
-                nc.vector.quantize_mx(
-                    out=xv_codes[:, d, :].bitcast(FP8X4),
-                    scales=xv_scales[:, d, :],
-                    in_=xv_grouped[:, d, :, :].rearrange("p n t -> p (n t)"),
-                )
-
             w10_codes = layer1.tile([P, in_passes, LIN_S], U32, align_bytes=64)
             w10_scales = layer1.tile([P, in_passes, LIN_S], U8, align_bytes=64)
             w11_codes = layer1.tile([P, 1, HID_V], U32, align_bytes=64)
             w11_scales = layer1.tile([P, 1, HID_V], U8, align_bytes=64)
-            gate1 = layer1.tile([P, v_passes, NODES, PACK], F32)
+            xs_codes = layer1.tile([P, in_passes, NODES], U32, align_bytes=64)
+            xs_scales = layer1.tile([P, in_passes, NODES], U8, align_bytes=64)
+            xv_codes = layer1.tile([P, DV, NODES], U32, align_bytes=64)
+            xv_scales = layer1.tile([P, DV, NODES], U8, align_bytes=64)
+
+            warm = layer1.tile([P, 1], F32)
+            nc.vector.memset(warm[:], 0.0)
+            nc.scalar.activation(out=warm[:], in_=warm[:], func=ACT.Silu)
+
+            quantise_weight_chunk(lin1_W1, 0, 0, w11_codes, w11_scales)
+
+            with tc.tile_pool(name="flip", bufs=1) as flip:
+                ident = flip.tile([P, P], BF16)
+                make_identity(nc, ident[:])
+                xs_grouped = flip.tile([P, in_passes, NODES, PACK], BF16, align_bytes=64)
+                xv_grouped = flip.tile([P, DV, NODES, PACK], BF16, align_bytes=64)
+                for nt in range(NODE_TILES):
+                    nodes = slice(nt * P, (nt + 1) * P)
+                    x_rows = flip.tile([P, IN_S + DV * IN_V], BF16, bufs=NODE_TILES)
+                    nc.sync.dma_start(out=x_rows[:], in_=features[nodes, :])
+                    for g in range(in_passes):
+                        flipped = psum_s.tile([P, PACK, P], BF16, tag="bank")
+                        for t in range(PACK):
+                            k0 = g * K_PASS + t * P
+                            nc.tensor.transpose(flipped[:, t, :], x_rows[:, k0 : k0 + P], ident[:])
+                        nc.scalar.copy(
+                            out=xs_grouped[:, g, nodes, :],
+                            in_=flipped[:].rearrange("p t n -> p n t"),
+                        )
+                    x_vec = x_rows[:, IN_S:].rearrange("n (i d) -> n d i", d=DV)
+                    for d in range(DV):
+                        flipped = psum_v.tile([P, PACK, P], BF16, tag="bank")
+                        for t in range(PACK):
+                            nc.tensor.transpose(
+                                flipped[:, t, :], x_vec[:, d, t * P : (t + 1) * P], ident[:]
+                            )
+                        nc.scalar.copy(
+                            out=xv_grouped[:, d, nodes, :],
+                            in_=flipped[:].rearrange("p t n -> p n t"),
+                        )
+                nc.vector.quantize_mx(
+                    out=xs_codes[:].rearrange("p g n -> p (g n)").bitcast(FP8X4),
+                    scales=xs_scales[:].rearrange("p g n -> p (g n)"),
+                    in_=xs_grouped[:].rearrange("p g n t -> p (g n t)"),
+                )
+                for d in range(DV):
+                    nc.vector.quantize_mx(
+                        out=xv_codes[:, d, :].bitcast(FP8X4),
+                        scales=xv_scales[:, d, :],
+                        in_=xv_grouped[:, d, :, :].rearrange("p n t -> p (n t)"),
+                    )
 
             def layer1_scalars(channel0, nt):
                 nodes = slice(nt * P, (nt + 1) * P)
@@ -155,68 +166,69 @@ def tile_feedforward_pa_kernel(tc, features, lin1_W0, lin1_W1, lin2_W0, lin2_W1,
                         )
                 return bank
 
-            for col0 in range(0, HID_S, CHUNK):
+            with tc.tile_pool(name="hidden", bufs=3) as hidden:
+                for col0 in range(0, HID_S, CHUNK):
+                    for g in range(in_passes):
+                        quantise_weight_chunk(lin1_W0, g, col0, w10_codes, w10_scales)
+                    for h in range(col0 // K_PASS, (col0 + CHUNK) // K_PASS):
+                        s_grouped = hidden.tile([P, NODES, PACK], BF16, align_bytes=64)
+                        for nt in range(NODE_TILES):
+                            bank = layer1_scalars(h * K_PASS, nt)
+                            nc.scalar.activation(
+                                out=s_grouped[:, nt * P : (nt + 1) * P, :],
+                                in_=bank[:].rearrange("p t n -> p n t"),
+                                func=ACT.Silu,
+                                scale=1.0 / math.sqrt(IN_S),
+                            )
+                        nc.vector.quantize_mx(
+                            out=g1s_codes[:, h, :].bitcast(FP8X4),
+                            scales=g1s_scales[:, h, :],
+                            in_=s_grouped[:].rearrange("p n t -> p (n t)"),
+                        )
+
+                gate1 = hidden.tile([P, v_passes, NODES, PACK], F32, bufs=1)
                 for g in range(in_passes):
-                    quantise_weight_chunk(lin1_W0, g, col0, w10_codes, w10_scales)
-                for h in range(col0 // K_PASS, (col0 + CHUNK) // K_PASS):
-                    s_grouped = layer1.tile([P, NODES, PACK], BF16, bufs=3, align_bytes=64)
+                    quantise_weight_chunk(lin1_W0, g, HID_S, w10_codes, w10_scales)
+                for h in range(v_passes):
                     for nt in range(NODE_TILES):
-                        bank = layer1_scalars(h * K_PASS, nt)
+                        bank = layer1_scalars(HID_S + h * K_PASS, nt)
                         nc.scalar.activation(
-                            out=s_grouped[:, nt * P : (nt + 1) * P, :],
+                            out=gate1[:, h, nt * P : (nt + 1) * P, :],
                             in_=bank[:].rearrange("p t n -> p n t"),
-                            func=ACT.Silu,
+                            func=ACT.Sigmoid,
                             scale=1.0 / math.sqrt(IN_S),
                         )
-                    nc.vector.quantize_mx(
-                        out=g1s_codes[:, h, :].bitcast(FP8X4),
-                        scales=g1s_scales[:, h, :],
-                        in_=s_grouped[:].rearrange("p n t -> p (n t)"),
-                    )
 
-            for g in range(in_passes):
-                quantise_weight_chunk(lin1_W0, g, HID_S, w10_codes, w10_scales)
-            for h in range(v_passes):
-                for nt in range(NODE_TILES):
-                    bank = layer1_scalars(HID_S + h * K_PASS, nt)
-                    nc.scalar.activation(
-                        out=gate1[:, h, nt * P : (nt + 1) * P, :],
-                        in_=bank[:].rearrange("p t n -> p n t"),
-                        func=ACT.Sigmoid,
-                        scale=1.0 / math.sqrt(IN_S),
-                    )
-
-            quantise_weight_chunk(lin1_W1, 0, 0, w11_codes, w11_scales)
-            for h in range(v_passes):
-                for d in range(DV):
-                    v_grouped = layer1.tile([P, NODES, PACK], BF16, bufs=3, align_bytes=64)
-                    for nt in range(NODE_TILES):
-                        nodes = slice(nt * P, (nt + 1) * P)
-                        bank = psum_v.tile([P, PACK, P], F32, tag="bank")
-                        for t in range(PACK):
-                            chans = slice(h * K_PASS + t * P, h * K_PASS + (t + 1) * P)
-                            mx(
-                                bank[:, t, :],
-                                w11_codes[:, 0, chans],
-                                w11_scales[:, 0, chans],
-                                xv_codes[:, d, nodes],
-                                xv_scales[:, d, nodes],
-                                start=True,
-                                stop=True,
+                for h in range(v_passes):
+                    for d in range(DV):
+                        v_grouped = hidden.tile([P, NODES, PACK], BF16, align_bytes=64)
+                        for nt in range(NODE_TILES):
+                            nodes = slice(nt * P, (nt + 1) * P)
+                            bank = psum_v.tile([P, PACK, P], F32, tag="bank")
+                            for t in range(PACK):
+                                chans = slice(h * K_PASS + t * P, h * K_PASS + (t + 1) * P)
+                                mx(
+                                    bank[:, t, :],
+                                    w11_codes[:, 0, chans],
+                                    w11_scales[:, 0, chans],
+                                    xv_codes[:, d, nodes],
+                                    xv_scales[:, d, nodes],
+                                    start=True,
+                                    stop=True,
+                                )
+                            nc.vector.scalar_tensor_tensor(
+                                out=v_grouped[:, nodes, :],
+                                in0=bank[:].rearrange("p t n -> p n t"),
+                                scalar=1.0 / math.sqrt(IN_V),
+                                in1=gate1[:, h, nodes, :],
+                                op0=ALU.mult,
+                                op1=ALU.mult,
                             )
-                        nc.vector.scalar_tensor_tensor(
-                            out=v_grouped[:, nodes, :],
-                            in0=bank[:].rearrange("p t n -> p n t"),
-                            scalar=1.0 / math.sqrt(IN_V),
-                            in1=gate1[:, h, nodes, :],
-                            op0=ALU.mult,
-                            op1=ALU.mult,
+                        nc.vector.quantize_mx(
+                            out=g1v_codes[:, h, d, :].bitcast(FP8X4),
+                            scales=g1v_scales[:, h, d, :],
+                            in_=v_grouped[:].rearrange("p n t -> p (n t)"),
                         )
-                    nc.vector.quantize_mx(
-                        out=g1v_codes[:, h, d, :].bitcast(FP8X4),
-                        scales=g1v_scales[:, h, d, :],
-                        in_=v_grouped[:].rearrange("p n t -> p (n t)"),
-                    )
 
         def layer2_scalars(col0):
             banks = [
@@ -225,10 +237,10 @@ def tile_feedforward_pa_kernel(tc, features, lin1_W0, lin1_W1, lin2_W0, lin2_W1,
             ]
             for h in range(s_passes):
                 quantise_weight_chunk(lin2_W0, h, col0, w20_codes, w20_scales)
-                for nt in range(NODE_TILES):
-                    nodes = slice(nt * P, (nt + 1) * P)
-                    for j in range(CHUNK // BANK):
-                        cols = slice(col0 + j * BANK, col0 + (j + 1) * BANK)
+                for j in range(CHUNK // BANK):
+                    cols = slice(col0 + j * BANK, col0 + (j + 1) * BANK)
+                    for nt in range(NODE_TILES):
+                        nodes = slice(nt * P, (nt + 1) * P)
                         mx(
                             banks[nt][j][:],
                             g1s_codes[:, h, nodes],
@@ -251,13 +263,12 @@ def tile_feedforward_pa_kernel(tc, features, lin1_W0, lin1_W1, lin2_W0, lin2_W1,
                 )
 
         with tc.tile_pool(name="layer2", bufs=3) as layer2:
-            for h in range(v_passes):
-                quantise_weight_chunk(lin2_W1, h, 0, w21_codes, w21_scales)
-            for nt in range(NODE_TILES):
+
+            def layer2_vectors(nt):
                 nodes = slice(nt * P, (nt + 1) * P)
-                for c0 in range(0, HID_V, BANK):
-                    v_out = layer2.tile([P, BANK, DV], F32)
-                    for c1 in range(0, BANK, P):
+                for c0 in range(0, HID_V, V_STORE):
+                    v_out = layer2.tile([P, V_STORE, DV], F32)
+                    for c1 in range(0, V_STORE, P):
                         chans = slice(c0 + c1, c0 + c1 + P)
                         bank = psum_v.tile([P, DV, P], F32, tag="bank")
                         for d in range(DV):
@@ -280,21 +291,28 @@ def tile_feedforward_pa_kernel(tc, features, lin1_W0, lin1_W1, lin2_W0, lin2_W1,
                             op1=ALU.mult,
                         )
                     nc.sync.dma_start(
-                        out=out[nodes, HID_S + DV * c0 : HID_S + DV * (c0 + BANK)],
+                        out=out[nodes, HID_S + DV * c0 : HID_S + DV * (c0 + V_STORE)],
                         in_=v_out[:].rearrange("p o d -> p (o d)"),
                     )
 
+            for h in range(v_passes):
+                quantise_weight_chunk(lin2_W1, h, 0, w21_codes, w21_scales)
+            layer2_vectors(0)
+
             for col0 in range(0, HID_S, CHUNK):
                 banks = layer2_scalars(col0)
-                for nt in range(NODE_TILES):
-                    s_out = layer2.tile([P, CHUNK], F32)
-                    for j in range(CHUNK // BANK):
+                for j in range(CHUNK // BANK):
+                    for nt in range(NODE_TILES):
+                        s_out = layer2.tile([P, BANK], F32)
                         nc.scalar.activation(
-                            out=s_out[:, j * BANK : (j + 1) * BANK],
+                            out=s_out[:],
                             in_=banks[nt][j][:],
                             func=ACT.Silu,
                             scale=1.0 / math.sqrt(HID_S),
                         )
-                    nc.sync.dma_start(
-                        out=out[nt * P : (nt + 1) * P, col0 : col0 + CHUNK], in_=s_out[:]
-                    )
+                        nc.sync.dma_start(
+                            out=out[nt * P : (nt + 1) * P, col0 + j * BANK : col0 + (j + 1) * BANK],
+                            in_=s_out[:],
+                        )
+
+            layer2_vectors(1)

@@ -26,7 +26,7 @@ HID_V = 1024
 LIN_S = HID_S + HID_V
 
 CHUNK = 1024
-HALF = CHUNK // 2
+PIECE = 256
 RUN = 4
 V_STORE = 512
 RAW_BUFS = 6
@@ -54,17 +54,20 @@ def tile_feedforward_pa_kernel(tc, features, lin1_W0, lin1_W1, lin2_W0, lin2_W1,
                     "(t p) w -> p t w", p=P
                 ),
             )
-            for half, copy in enumerate((nc.vector.tensor_copy, nc.scalar.copy)):
-                grouped = stream.tile(
-                    [P, HALF, PACK], BF16, name="grouped%d" % half, bufs=3, align_bytes=64
-                )
+            def regroup(copy, name, first, width):
+                grouped = stream.tile([P, width, PACK], BF16, name=name, bufs=3, align_bytes=64)
                 copy(
                     out=grouped[:].rearrange("p (c i) t -> p c t i", i=RUN),
-                    in_=raw[:, :, half * HALF : (half + 1) * HALF].rearrange(
-                        "p t (c i) -> p c t i", i=RUN
-                    ),
+                    in_=raw[:, :, first : first + width].rearrange("p t (c i) -> p c t i", i=RUN),
                 )
-                cols = slice(col0 + half * HALF, col0 + (half + 1) * HALF)
+                return grouped, slice(col0 + first, col0 + first + width)
+
+            pieces = [
+                regroup(nc.vector.tensor_copy, "grouped_a", 0, PIECE),
+                regroup(nc.vector.tensor_copy, "grouped_b", PIECE, PIECE),
+                regroup(nc.scalar.copy, "grouped_s", 2 * PIECE, 2 * PIECE),
+            ]
+            for grouped, cols in pieces:
                 nc.vector.quantize_mx(
                     out=codes[:, g, cols].bitcast(FP8X4),
                     scales=scales[:, g, cols],
@@ -199,9 +202,13 @@ def tile_feedforward_pa_kernel(tc, features, lin1_W0, lin1_W1, lin2_W0, lin2_W1,
                             scale=1.0 / math.sqrt(IN_S),
                         )
 
-                for h in range(v_passes):
-                    for d in range(DV):
-                        v_grouped = hidden.tile([P, NODES, PACK], BF16, align_bytes=64)
+                v_grouped = []
+                for u in range(v_passes * DV + 1):
+                    if u < v_passes * DV:
+                        h, d = divmod(u, DV)
+                        v_grouped.append(
+                            hidden.tile([P, NODES, PACK], BF16, name="v_grouped", align_bytes=64)
+                        )
                         for nt in range(NODE_TILES):
                             nodes = slice(nt * P, (nt + 1) * P)
                             bank = psum_v.tile([P, PACK, P], F32, tag="bank")
@@ -217,17 +224,19 @@ def tile_feedforward_pa_kernel(tc, features, lin1_W0, lin1_W1, lin2_W0, lin2_W1,
                                     stop=True,
                                 )
                             nc.vector.scalar_tensor_tensor(
-                                out=v_grouped[:, nodes, :],
+                                out=v_grouped[u][:, nodes, :],
                                 in0=bank[:].rearrange("p t n -> p n t"),
                                 scalar=1.0 / math.sqrt(IN_V),
                                 in1=gate1[:, h, nodes, :],
                                 op0=ALU.mult,
                                 op1=ALU.mult,
                             )
+                    if u > 0:
+                        h, d = divmod(u - 1, DV)
                         nc.vector.quantize_mx(
                             out=g1v_codes[:, h, d, :].bitcast(FP8X4),
                             scales=g1v_scales[:, h, d, :],
-                            in_=v_grouped[:].rearrange("p n t -> p (n t)"),
+                            in_=v_grouped[u - 1][:].rearrange("p n t -> p (n t)"),
                         )
 
         def layer2_scalars(col0):

@@ -26,12 +26,25 @@ HID_V = 1024
 LIN_S = HID_S + HID_V
 
 CHUNK = 1024
-PIECE = 256
+VECTOR_COLS = 512
+VECTOR_COLS_GATING = 384
 RUN = 4
-V_STORE = 512
+V_STORE = 256
 RAW_BUFS = 6
+GROUPED_BUFS = 3
 
 FLOPS = 2 * NODES * (IN_S + HID_S) * LIN_S + 2 * NODES * DV * (IN_V + HID_V) * HID_V
+
+
+def aligned_blocks(first, end):
+    blocks = []
+    while first < end:
+        size = CHUNK
+        while first % size != 0 or first + size > end:
+            size //= 2
+        blocks.append((first, size))
+        first += size
+    return blocks
 
 
 def tile_feedforward_pa_kernel(tc, features, lin1_W0, lin1_W1, lin2_W0, lin2_W1, out):
@@ -46,7 +59,7 @@ def tile_feedforward_pa_kernel(tc, features, lin1_W0, lin1_W1, lin2_W0, lin2_W1,
         name="psum_v", bufs=4
     ) as psum_v:
 
-        def quantise_weight_chunk(w, g, col0, codes, scales):
+        def quantise_weight_chunk(w, g, col0, codes, scales, vector_cols):
             raw = stream.tile([P, PACK, CHUNK], BF16, bufs=RAW_BUFS)
             nc.sync.dma_start(
                 out=raw[:],
@@ -54,25 +67,26 @@ def tile_feedforward_pa_kernel(tc, features, lin1_W0, lin1_W1, lin2_W0, lin2_W1,
                     "(t p) w -> p t w", p=P
                 ),
             )
-            def regroup(copy, name, first, width):
-                grouped = stream.tile([P, width, PACK], BF16, name=name, bufs=3, align_bytes=64)
+            parts = (
+                (nc.vector.tensor_copy, "grouped_v", 0, vector_cols),
+                (nc.scalar.copy, "grouped_s", vector_cols, CHUNK),
+            )
+            for copy, name, first, end in parts:
+                grouped = stream.tile(
+                    [P, end - first, PACK], BF16, name=name, bufs=GROUPED_BUFS, align_bytes=64
+                )
                 copy(
                     out=grouped[:].rearrange("p (c i) t -> p c t i", i=RUN),
-                    in_=raw[:, :, first : first + width].rearrange("p t (c i) -> p c t i", i=RUN),
+                    in_=raw[:, :, first:end].rearrange("p t (c i) -> p c t i", i=RUN),
                 )
-                return grouped, slice(col0 + first, col0 + first + width)
-
-            pieces = [
-                regroup(nc.vector.tensor_copy, "grouped_a", 0, PIECE),
-                regroup(nc.vector.tensor_copy, "grouped_b", PIECE, PIECE),
-                regroup(nc.scalar.copy, "grouped_s", 2 * PIECE, 2 * PIECE),
-            ]
-            for grouped, cols in pieces:
-                nc.vector.quantize_mx(
-                    out=codes[:, g, cols].bitcast(FP8X4),
-                    scales=scales[:, g, cols],
-                    in_=grouped[:].rearrange("p w t -> p (w t)"),
-                )
+                for col, size in aligned_blocks(first, end):
+                    nc.vector.quantize_mx(
+                        out=codes[:, col : col + size].bitcast(FP8X4),
+                        scales=scales[:, col : col + size],
+                        in_=grouped[:, col - first : col - first + size, :].rearrange(
+                            "p w t -> p (w t)"
+                        ),
+                    )
 
         def mx(acc, a_codes, a_scales, b_codes, b_scales, start, stop):
             nc.tensor.matmul_mx(
@@ -85,21 +99,19 @@ def tile_feedforward_pa_kernel(tc, features, lin1_W0, lin1_W1, lin2_W0, lin2_W1,
                 stop=stop,
             )
 
-        w20_codes = keep.tile([P, s_passes, LIN_S], U32, align_bytes=64)
-        w20_scales = keep.tile([P, s_passes, LIN_S], U8, align_bytes=64)
-        w21_codes = keep.tile([P, v_passes, HID_V], U32, align_bytes=64)
-        w21_scales = keep.tile([P, v_passes, HID_V], U8, align_bytes=64)
         g1s_codes = keep.tile([P, s_passes, NODES], U32, align_bytes=64)
         g1s_scales = keep.tile([P, s_passes, NODES], U8, align_bytes=64)
         g1v_codes = keep.tile([P, v_passes, DV, NODES], U32, align_bytes=64)
         g1v_scales = keep.tile([P, v_passes, DV, NODES], U8, align_bytes=64)
+        w21_codes = keep.tile([P, v_passes, HID_V], U32, align_bytes=64)
+        w21_scales = keep.tile([P, v_passes, HID_V], U8, align_bytes=64)
         gate2 = keep.tile([P, NODE_TILES, HID_V], F32)
 
         with tc.tile_pool(name="layer1", bufs=1) as layer1:
             w10_codes = layer1.tile([P, in_passes, LIN_S], U32, align_bytes=64)
             w10_scales = layer1.tile([P, in_passes, LIN_S], U8, align_bytes=64)
-            w11_codes = layer1.tile([P, 1, HID_V], U32, align_bytes=64)
-            w11_scales = layer1.tile([P, 1, HID_V], U8, align_bytes=64)
+            w11_codes = layer1.tile([P, HID_V], U32, align_bytes=64)
+            w11_scales = layer1.tile([P, HID_V], U8, align_bytes=64)
             xs_codes = layer1.tile([P, in_passes, NODES], U32, align_bytes=64)
             xs_scales = layer1.tile([P, in_passes, NODES], U8, align_bytes=64)
             xv_codes = layer1.tile([P, DV, NODES], U32, align_bytes=64)
@@ -109,7 +121,7 @@ def tile_feedforward_pa_kernel(tc, features, lin1_W0, lin1_W1, lin2_W0, lin2_W1,
             nc.vector.memset(warm[:], 0.0)
             nc.scalar.activation(out=warm[:], in_=warm[:], func=ACT.Silu)
 
-            quantise_weight_chunk(lin1_W1, 0, 0, w11_codes, w11_scales)
+            quantise_weight_chunk(lin1_W1, 0, 0, w11_codes, w11_scales, VECTOR_COLS)
 
             with tc.tile_pool(name="flip", bufs=1) as flip:
                 ident = flip.tile([P, P], BF16)
@@ -125,7 +137,7 @@ def tile_feedforward_pa_kernel(tc, features, lin1_W0, lin1_W1, lin2_W0, lin2_W1,
                         for t in range(PACK):
                             k0 = g * K_PASS + t * P
                             nc.tensor.transpose(flipped[:, t, :], x_rows[:, k0 : k0 + P], ident[:])
-                        nc.scalar.copy(
+                        nc.vector.tensor_copy(
                             out=xs_grouped[:, g, nodes, :],
                             in_=flipped[:].rearrange("p t n -> p n t"),
                         )
@@ -152,6 +164,13 @@ def tile_feedforward_pa_kernel(tc, features, lin1_W0, lin1_W1, lin2_W0, lin2_W1,
                         in_=xv_grouped[:, d, :, :].rearrange("p n t -> p (n t)"),
                     )
 
+            def layer1_weights(col0):
+                for g in range(in_passes):
+                    cols = slice(col0, col0 + CHUNK)
+                    quantise_weight_chunk(
+                        lin1_W0, g, col0, w10_codes[:, g, cols], w10_scales[:, g, cols], VECTOR_COLS
+                    )
+
             def layer1_scalars(channel0, nt):
                 nodes = slice(nt * P, (nt + 1) * P)
                 bank = psum_s.tile([P, PACK, P], F32, tag="bank")
@@ -171,8 +190,7 @@ def tile_feedforward_pa_kernel(tc, features, lin1_W0, lin1_W1, lin2_W0, lin2_W1,
 
             with tc.tile_pool(name="hidden", bufs=3) as hidden:
                 for col0 in range(0, HID_S, CHUNK):
-                    for g in range(in_passes):
-                        quantise_weight_chunk(lin1_W0, g, col0, w10_codes, w10_scales)
+                    layer1_weights(col0)
                     for h in range(col0 // K_PASS, (col0 + CHUNK) // K_PASS):
                         s_grouped = hidden.tile([P, NODES, PACK], BF16, align_bytes=64)
                         for nt in range(NODE_TILES):
@@ -190,8 +208,7 @@ def tile_feedforward_pa_kernel(tc, features, lin1_W0, lin1_W1, lin2_W0, lin2_W1,
                         )
 
                 gate1 = hidden.tile([P, v_passes, NODES, PACK], F32, bufs=1)
-                for g in range(in_passes):
-                    quantise_weight_chunk(lin1_W0, g, HID_S, w10_codes, w10_scales)
+                layer1_weights(HID_S)
                 for h in range(v_passes):
                     for nt in range(NODE_TILES):
                         bank = layer1_scalars(HID_S + h * K_PASS, nt)
@@ -202,13 +219,9 @@ def tile_feedforward_pa_kernel(tc, features, lin1_W0, lin1_W1, lin2_W0, lin2_W1,
                             scale=1.0 / math.sqrt(IN_S),
                         )
 
-                v_grouped = []
-                for u in range(v_passes * DV + 1):
-                    if u < v_passes * DV:
-                        h, d = divmod(u, DV)
-                        v_grouped.append(
-                            hidden.tile([P, NODES, PACK], BF16, name="v_grouped", align_bytes=64)
-                        )
+                for h in range(v_passes):
+                    for d in range(DV):
+                        v_grouped = hidden.tile([P, NODES, PACK], BF16, align_bytes=64)
                         for nt in range(NODE_TILES):
                             nodes = slice(nt * P, (nt + 1) * P)
                             bank = psum_v.tile([P, PACK, P], F32, tag="bank")
@@ -216,52 +229,52 @@ def tile_feedforward_pa_kernel(tc, features, lin1_W0, lin1_W1, lin2_W0, lin2_W1,
                                 chans = slice(h * K_PASS + t * P, h * K_PASS + (t + 1) * P)
                                 mx(
                                     bank[:, t, :],
-                                    w11_codes[:, 0, chans],
-                                    w11_scales[:, 0, chans],
+                                    w11_codes[:, chans],
+                                    w11_scales[:, chans],
                                     xv_codes[:, d, nodes],
                                     xv_scales[:, d, nodes],
                                     start=True,
                                     stop=True,
                                 )
                             nc.vector.scalar_tensor_tensor(
-                                out=v_grouped[u][:, nodes, :],
+                                out=v_grouped[:, nodes, :],
                                 in0=bank[:].rearrange("p t n -> p n t"),
                                 scalar=1.0 / math.sqrt(IN_V),
                                 in1=gate1[:, h, nodes, :],
                                 op0=ALU.mult,
                                 op1=ALU.mult,
                             )
-                    if u > 0:
-                        h, d = divmod(u - 1, DV)
                         nc.vector.quantize_mx(
                             out=g1v_codes[:, h, d, :].bitcast(FP8X4),
                             scales=g1v_scales[:, h, d, :],
-                            in_=v_grouped[u - 1][:].rearrange("p n t -> p (n t)"),
+                            in_=v_grouped[:].rearrange("p n t -> p (n t)"),
                         )
 
-        def layer2_scalars(col0):
+        def layer2_scalars(col0, vector_cols):
             banks = [
                 [psum_s.tile([P, BANK], F32, name="acc", tag="bank") for j in range(CHUNK // BANK)]
                 for nt in range(NODE_TILES)
             ]
             for h in range(s_passes):
-                quantise_weight_chunk(lin2_W0, h, col0, w20_codes, w20_scales)
+                w20_codes = stream.tile([P, CHUNK], U32, bufs=12, align_bytes=64)
+                w20_scales = stream.tile([P, CHUNK], U8, bufs=12, align_bytes=64)
+                quantise_weight_chunk(lin2_W0, h, col0, w20_codes, w20_scales, vector_cols)
                 for j in range(CHUNK // BANK):
-                    cols = slice(col0 + j * BANK, col0 + (j + 1) * BANK)
+                    cols = slice(j * BANK, (j + 1) * BANK)
                     for nt in range(NODE_TILES):
                         nodes = slice(nt * P, (nt + 1) * P)
                         mx(
                             banks[nt][j][:],
                             g1s_codes[:, h, nodes],
                             g1s_scales[:, h, nodes],
-                            w20_codes[:, h, cols],
-                            w20_scales[:, h, cols],
+                            w20_codes[:, cols],
+                            w20_scales[:, cols],
                             start=(h == 0),
                             stop=(h == s_passes - 1),
                         )
             return banks
 
-        banks = layer2_scalars(HID_S)
+        banks = layer2_scalars(HID_S, VECTOR_COLS_GATING)
         for nt in range(NODE_TILES):
             for j in range(CHUNK // BANK):
                 nc.scalar.activation(
@@ -271,12 +284,12 @@ def tile_feedforward_pa_kernel(tc, features, lin1_W0, lin1_W1, lin2_W0, lin2_W1,
                     scale=1.0 / math.sqrt(HID_S),
                 )
 
-        with tc.tile_pool(name="layer2", bufs=3) as layer2:
+        with tc.tile_pool(name="layer2", bufs=8) as layer2:
 
             def layer2_vectors(nt):
                 nodes = slice(nt * P, (nt + 1) * P)
                 for c0 in range(0, HID_V, V_STORE):
-                    v_out = layer2.tile([P, V_STORE, DV], F32)
+                    v_out = layer2.tile([P, V_STORE, DV], F32, bufs=4)
                     for c1 in range(0, V_STORE, P):
                         chans = slice(c0 + c1, c0 + c1 + P)
                         bank = psum_v.tile([P, DV, P], F32, tag="bank")
@@ -305,11 +318,13 @@ def tile_feedforward_pa_kernel(tc, features, lin1_W0, lin1_W1, lin2_W0, lin2_W1,
                     )
 
             for h in range(v_passes):
-                quantise_weight_chunk(lin2_W1, h, 0, w21_codes, w21_scales)
+                quantise_weight_chunk(
+                    lin2_W1, h, 0, w21_codes[:, h, :], w21_scales[:, h, :], VECTOR_COLS_GATING
+                )
             layer2_vectors(0)
 
             for col0 in range(0, HID_S, CHUNK):
-                banks = layer2_scalars(col0)
+                banks = layer2_scalars(col0, VECTOR_COLS_GATING if col0 == 0 else VECTOR_COLS)
                 for j in range(CHUNK // BANK):
                     for nt in range(NODE_TILES):
                         s_out = layer2.tile([P, BANK], F32)

@@ -28,6 +28,7 @@ LIN_S = HID_S + HID_V
 CHUNK = 1024
 VECTOR_COLS = 512
 VECTOR_COLS_GATING = 384
+TENSOR_COLS = 256
 RUN = 4
 V_STORE = 256
 RAW_BUFS = 6
@@ -56,8 +57,10 @@ def tile_feedforward_pa_kernel(tc, features, lin1_W0, lin1_W1, lin2_W0, lin2_W1,
     with tc.tile_pool(name="keep", bufs=1) as keep, tc.tile_pool(
         name="stream", bufs=1
     ) as stream, tc.psum_pool(name="psum_s", bufs=4) as psum_s, tc.psum_pool(
-        name="psum_v", bufs=4
-    ) as psum_v:
+        name="psum_v", bufs=2
+    ) as psum_v, tc.psum_pool(name="psum_w", bufs=2) as psum_w:
+        ident = keep.tile([P, P], BF16)
+        make_identity(nc, ident[:])
 
         def quantise_weight_chunk(w, g, col0, codes, scales, vector_cols):
             raw = stream.tile([P, PACK, CHUNK], BF16, bufs=RAW_BUFS)
@@ -67,18 +70,32 @@ def tile_feedforward_pa_kernel(tc, features, lin1_W0, lin1_W1, lin2_W0, lin2_W1,
                     "(t p) w -> p t w", p=P
                 ),
             )
+            turned = psum_w.tile([P, TENSOR_COLS, PACK], BF16, tag="turned")
+            for c0 in range(0, TENSOR_COLS, P):
+                nc.tensor.matmul(
+                    turned[:, c0 : c0 + P, :],
+                    ident[:],
+                    raw[:, :, c0 : c0 + P].rearrange("p t c -> p c t"),
+                    start=True,
+                    stop=True,
+                )
+            first_s = TENSOR_COLS + vector_cols
             parts = (
-                (nc.vector.tensor_copy, "grouped_v", 0, vector_cols),
-                (nc.scalar.copy, "grouped_s", vector_cols, CHUNK),
+                (nc.scalar.copy, "grouped_t", 0, TENSOR_COLS),
+                (nc.vector.tensor_copy, "grouped_v", TENSOR_COLS, first_s),
+                (nc.scalar.copy, "grouped_s", first_s, CHUNK),
             )
             for copy, name, first, end in parts:
                 grouped = stream.tile(
                     [P, end - first, PACK], BF16, name=name, bufs=GROUPED_BUFS, align_bytes=64
                 )
-                copy(
-                    out=grouped[:].rearrange("p (c i) t -> p c t i", i=RUN),
-                    in_=raw[:, :, first:end].rearrange("p t (c i) -> p c t i", i=RUN),
-                )
+                if first == 0:
+                    copy(out=grouped[:], in_=turned[:])
+                else:
+                    copy(
+                        out=grouped[:].rearrange("p (c i) t -> p c t i", i=RUN),
+                        in_=raw[:, :, first:end].rearrange("p t (c i) -> p c t i", i=RUN),
+                    )
                 for col, size in aligned_blocks(first, end):
                     nc.vector.quantize_mx(
                         out=codes[:, col : col + size].bitcast(FP8X4),
@@ -124,8 +141,6 @@ def tile_feedforward_pa_kernel(tc, features, lin1_W0, lin1_W1, lin2_W0, lin2_W1,
             quantise_weight_chunk(lin1_W1, 0, 0, w11_codes, w11_scales, VECTOR_COLS)
 
             with tc.tile_pool(name="flip", bufs=1) as flip:
-                ident = flip.tile([P, P], BF16)
-                make_identity(nc, ident[:])
                 xs_grouped = flip.tile([P, in_passes, NODES, PACK], BF16, align_bytes=64)
                 xv_grouped = flip.tile([P, DV, NODES, PACK], BF16, align_bytes=64)
                 for nt in range(NODE_TILES):
@@ -215,9 +230,18 @@ def tile_feedforward_pa_kernel(tc, features, lin1_W0, lin1_W1, lin2_W0, lin2_W1,
                         nc.scalar.activation(
                             out=gate1[:, h, nt * P : (nt + 1) * P, :],
                             in_=bank[:].rearrange("p t n -> p n t"),
-                            func=ACT.Sigmoid,
-                            scale=1.0 / math.sqrt(IN_S),
+                            func=ACT.Tanh,
+                            scale=0.5 / math.sqrt(IN_S),
                         )
+                    gate_h = gate1[:, h, :, :].rearrange("p n t -> p (n t)")
+                    nc.vector.tensor_scalar(
+                        out=gate_h,
+                        in0=gate_h,
+                        scalar1=0.5 / math.sqrt(IN_V),
+                        scalar2=0.5 / math.sqrt(IN_V),
+                        op0=ALU.mult,
+                        op1=ALU.add,
+                    )
 
                 for h in range(v_passes):
                     for d in range(DV):
@@ -236,13 +260,11 @@ def tile_feedforward_pa_kernel(tc, features, lin1_W0, lin1_W1, lin2_W0, lin2_W1,
                                     start=True,
                                     stop=True,
                                 )
-                            nc.vector.scalar_tensor_tensor(
+                            nc.vector.tensor_tensor(
                                 out=v_grouped[:, nodes, :],
                                 in0=bank[:].rearrange("p t n -> p n t"),
-                                scalar=1.0 / math.sqrt(IN_V),
                                 in1=gate1[:, h, nodes, :],
-                                op0=ALU.mult,
-                                op1=ALU.mult,
+                                op=ALU.mult,
                             )
                         nc.vector.quantize_mx(
                             out=g1v_codes[:, h, d, :].bitcast(FP8X4),
@@ -280,9 +302,17 @@ def tile_feedforward_pa_kernel(tc, features, lin1_W0, lin1_W1, lin2_W0, lin2_W1,
                 nc.scalar.activation(
                     out=gate2[:, nt, j * BANK : (j + 1) * BANK],
                     in_=banks[nt][j][:],
-                    func=ACT.Sigmoid,
-                    scale=1.0 / math.sqrt(HID_S),
+                    func=ACT.Tanh,
+                    scale=0.5 / math.sqrt(HID_S),
                 )
+            nc.vector.tensor_scalar(
+                out=gate2[:, nt, :],
+                in0=gate2[:, nt, :],
+                scalar1=0.5 / math.sqrt(HID_V),
+                scalar2=0.5 / math.sqrt(HID_V),
+                op0=ALU.mult,
+                op1=ALU.add,
+            )
 
         with tc.tile_pool(name="layer2", bufs=8) as layer2:
 
@@ -304,13 +334,11 @@ def tile_feedforward_pa_kernel(tc, features, lin1_W0, lin1_W1, lin2_W0, lin2_W1,
                                     start=(h == 0),
                                     stop=(h == v_passes - 1),
                                 )
-                        nc.vector.scalar_tensor_tensor(
+                        nc.vector.tensor_tensor(
                             out=v_out[:, c1 : c1 + P, :],
                             in0=bank[:].rearrange("p d o -> p o d"),
-                            scalar=1.0 / math.sqrt(HID_V),
                             in1=gate2[:, nt, chans].unsqueeze(2).to_broadcast([P, P, DV]),
-                            op0=ALU.mult,
-                            op1=ALU.mult,
+                            op=ALU.mult,
                         )
                     nc.sync.dma_start(
                         out=out[nodes, HID_S + DV * c0 : HID_S + DV * (c0 + V_STORE)],

@@ -26,26 +26,15 @@ HID_V = 1024
 LIN_S = HID_S + HID_V
 
 CHUNK = 1024
-VECTOR_COLS = 512
-VECTOR_COLS_GATING = 384
+VECTOR_COLS = 384
 TENSOR_COLS = 256
 RUN = 4
 V_STORE = 256
 RAW_BUFS = 6
-GROUPED_BUFS = 3
+LOAD_AHEAD = 5
+GROUPED_BUFS = 4
 
 FLOPS = 2 * NODES * (IN_S + HID_S) * LIN_S + 2 * NODES * DV * (IN_V + HID_V) * HID_V
-
-
-def aligned_blocks(first, end):
-    blocks = []
-    while first < end:
-        size = CHUNK
-        while first % size != 0 or first + size > end:
-            size //= 2
-        blocks.append((first, size))
-        first += size
-    return blocks
 
 
 def tile_feedforward_pa_kernel(tc, features, lin1_W0, lin1_W1, lin2_W0, lin2_W1, out):
@@ -62,7 +51,7 @@ def tile_feedforward_pa_kernel(tc, features, lin1_W0, lin1_W1, lin2_W0, lin2_W1,
         ident = keep.tile([P, P], BF16)
         make_identity(nc, ident[:])
 
-        def quantise_weight_chunk(w, g, col0, codes, scales, vector_cols):
+        def load_chunk(w, g, col0):
             raw = stream.tile([P, PACK, CHUNK], BF16, bufs=RAW_BUFS)
             nc.sync.dma_start(
                 out=raw[:],
@@ -70,6 +59,10 @@ def tile_feedforward_pa_kernel(tc, features, lin1_W0, lin1_W1, lin2_W0, lin2_W1,
                     "(t p) w -> p t w", p=P
                 ),
             )
+            return raw
+
+        def regroup_chunk(raw):
+            grouped = stream.tile([P, CHUNK, PACK], BF16, bufs=GROUPED_BUFS, align_bytes=64)
             turned = psum_w.tile([P, TENSOR_COLS, PACK], BF16, tag="turned")
             for c0 in range(0, TENSOR_COLS, P):
                 nc.tensor.matmul(
@@ -79,31 +72,51 @@ def tile_feedforward_pa_kernel(tc, features, lin1_W0, lin1_W1, lin2_W0, lin2_W1,
                     start=True,
                     stop=True,
                 )
-            first_s = TENSOR_COLS + vector_cols
-            parts = (
-                (nc.scalar.copy, "grouped_t", 0, TENSOR_COLS),
-                (nc.vector.tensor_copy, "grouped_v", TENSOR_COLS, first_s),
-                (nc.scalar.copy, "grouped_s", first_s, CHUNK),
-            )
-            for copy, name, first, end in parts:
-                grouped = stream.tile(
-                    [P, end - first, PACK], BF16, name=name, bufs=GROUPED_BUFS, align_bytes=64
+            first_v = CHUNK - VECTOR_COLS
+            for copy, first, end in (
+                (nc.vector.tensor_copy, first_v, CHUNK),
+                (nc.scalar.copy, TENSOR_COLS, first_v),
+            ):
+                copy(
+                    out=grouped[:, first:end, :].rearrange("p (c i) t -> p c t i", i=RUN),
+                    in_=raw[:, :, first:end].rearrange("p t (c i) -> p c t i", i=RUN),
                 )
-                if first == 0:
-                    copy(out=grouped[:], in_=turned[:])
-                else:
-                    copy(
-                        out=grouped[:].rearrange("p (c i) t -> p c t i", i=RUN),
-                        in_=raw[:, :, first:end].rearrange("p t (c i) -> p c t i", i=RUN),
-                    )
-                for col, size in aligned_blocks(first, end):
-                    nc.vector.quantize_mx(
-                        out=codes[:, col : col + size].bitcast(FP8X4),
-                        scales=scales[:, col : col + size],
-                        in_=grouped[:, col - first : col - first + size, :].rearrange(
-                            "p w t -> p (w t)"
-                        ),
-                    )
+            nc.scalar.copy(out=grouped[:, :TENSOR_COLS, :], in_=turned[:])
+            return grouped
+
+        def quantise_chunk(grouped, codes, scales):
+            nc.vector.quantize_mx(
+                out=codes.bitcast(FP8X4),
+                scales=scales,
+                in_=grouped[:].rearrange("p w t -> p (w t)"),
+            )
+
+        chunks = (
+            [(lin1_W1, 0, 0)]
+            + [(lin1_W0, g, c) for c in range(0, LIN_S, CHUNK) for g in range(in_passes)]
+            + [(lin2_W0, h, HID_S) for h in range(s_passes)]
+            + [(lin2_W1, h, 0) for h in range(v_passes)]
+            + [(lin2_W0, h, c) for c in range(0, HID_S, CHUNK) for h in range(s_passes)]
+        )
+        raws = []
+        regrouped = []
+        quantised = []
+
+        def load_until(n):
+            while len(raws) < min(n, len(chunks)):
+                raws.append(load_chunk(*chunks[len(raws)]))
+
+        def regroup_until(n):
+            while len(regrouped) < min(n, len(chunks)):
+                load_until(len(regrouped) + 1)
+                regrouped.append(regroup_chunk(raws[len(regrouped)]))
+
+        def next_weight_chunk(codes, scales):
+            i = len(quantised)
+            load_until(i + 1 + LOAD_AHEAD)
+            regroup_until(i + 2)
+            quantise_chunk(regrouped[i], codes, scales)
+            quantised.append(i)
 
         def mx(acc, a_codes, a_scales, b_codes, b_scales, start, stop):
             nc.tensor.matmul_mx(
@@ -138,7 +151,8 @@ def tile_feedforward_pa_kernel(tc, features, lin1_W0, lin1_W1, lin2_W0, lin2_W1,
             nc.vector.memset(warm[:], 0.0)
             nc.scalar.activation(out=warm[:], in_=warm[:], func=ACT.Silu)
 
-            quantise_weight_chunk(lin1_W1, 0, 0, w11_codes, w11_scales, VECTOR_COLS)
+            load_until(1)
+            regroup_until(1)
 
             with tc.tile_pool(name="flip", bufs=1) as flip:
                 xs_grouped = flip.tile([P, in_passes, NODES, PACK], BF16, align_bytes=64)
@@ -179,12 +193,12 @@ def tile_feedforward_pa_kernel(tc, features, lin1_W0, lin1_W1, lin2_W0, lin2_W1,
                         in_=xv_grouped[:, d, :, :].rearrange("p n t -> p (n t)"),
                     )
 
+            next_weight_chunk(w11_codes[:], w11_scales[:])
+
             def layer1_weights(col0):
                 for g in range(in_passes):
                     cols = slice(col0, col0 + CHUNK)
-                    quantise_weight_chunk(
-                        lin1_W0, g, col0, w10_codes[:, g, cols], w10_scales[:, g, cols], VECTOR_COLS
-                    )
+                    next_weight_chunk(w10_codes[:, g, cols], w10_scales[:, g, cols])
 
             def layer1_scalars(channel0, nt):
                 nodes = slice(nt * P, (nt + 1) * P)
@@ -272,7 +286,7 @@ def tile_feedforward_pa_kernel(tc, features, lin1_W0, lin1_W1, lin2_W0, lin2_W1,
                             in_=v_grouped[:].rearrange("p n t -> p (n t)"),
                         )
 
-        def layer2_scalars(col0, vector_cols):
+        def layer2_scalars():
             banks = [
                 [psum_s.tile([P, BANK], F32, name="acc", tag="bank") for j in range(CHUNK // BANK)]
                 for nt in range(NODE_TILES)
@@ -280,7 +294,7 @@ def tile_feedforward_pa_kernel(tc, features, lin1_W0, lin1_W1, lin2_W0, lin2_W1,
             for h in range(s_passes):
                 w20_codes = stream.tile([P, CHUNK], U32, bufs=12, align_bytes=64)
                 w20_scales = stream.tile([P, CHUNK], U8, bufs=12, align_bytes=64)
-                quantise_weight_chunk(lin2_W0, h, col0, w20_codes, w20_scales, vector_cols)
+                next_weight_chunk(w20_codes[:], w20_scales[:])
                 for j in range(CHUNK // BANK):
                     cols = slice(j * BANK, (j + 1) * BANK)
                     for nt in range(NODE_TILES):
@@ -296,7 +310,7 @@ def tile_feedforward_pa_kernel(tc, features, lin1_W0, lin1_W1, lin2_W0, lin2_W1,
                         )
             return banks
 
-        banks = layer2_scalars(HID_S, VECTOR_COLS_GATING)
+        banks = layer2_scalars()
         for nt in range(NODE_TILES):
             for j in range(CHUNK // BANK):
                 nc.scalar.activation(
@@ -346,13 +360,11 @@ def tile_feedforward_pa_kernel(tc, features, lin1_W0, lin1_W1, lin2_W0, lin2_W1,
                     )
 
             for h in range(v_passes):
-                quantise_weight_chunk(
-                    lin2_W1, h, 0, w21_codes[:, h, :], w21_scales[:, h, :], VECTOR_COLS_GATING
-                )
+                next_weight_chunk(w21_codes[:, h, :], w21_scales[:, h, :])
             layer2_vectors(0)
 
             for col0 in range(0, HID_S, CHUNK):
-                banks = layer2_scalars(col0, VECTOR_COLS_GATING if col0 == 0 else VECTOR_COLS)
+                banks = layer2_scalars()
                 for j in range(CHUNK // BANK):
                     for nt in range(NODE_TILES):
                         s_out = layer2.tile([P, BANK], F32)

@@ -26,13 +26,16 @@ HID_V = 1024
 LIN_S = HID_S + HID_V
 
 CHUNK = 1024
-VECTOR_COLS = 384
-TENSOR_COLS = 256
+VECTOR_COLS_EARLY = 640
+VECTOR_COLS = 448
+LAST_PARTS = 2
 RUN = 4
 V_STORE = 256
-RAW_BUFS = 6
-LOAD_AHEAD = 5
-GROUPED_BUFS = 4
+RAW_BUFS = 7
+LOAD_AHEAD = 6
+REGROUP_AHEAD = 2
+GROUPED_BUFS = 5
+W20_BUFS = 6
 
 FLOPS = 2 * NODES * (IN_S + HID_S) * LIN_S + 2 * NODES * DV * (IN_V + HID_V) * HID_V
 
@@ -46,75 +49,73 @@ def tile_feedforward_pa_kernel(tc, features, lin1_W0, lin1_W1, lin2_W0, lin2_W1,
     with tc.tile_pool(name="keep", bufs=1) as keep, tc.tile_pool(
         name="stream", bufs=1
     ) as stream, tc.psum_pool(name="psum_s", bufs=4) as psum_s, tc.psum_pool(
-        name="psum_v", bufs=2
-    ) as psum_v, tc.psum_pool(name="psum_w", bufs=2) as psum_w:
-        ident = keep.tile([P, P], BF16)
-        make_identity(nc, ident[:])
+        name="psum_v", bufs=4
+    ) as psum_v:
 
-        def load_chunk(w, g, col0):
+        def load(w, g, col0, cols):
             raw = stream.tile([P, PACK, CHUNK], BF16, bufs=RAW_BUFS)
             nc.sync.dma_start(
-                out=raw[:],
-                in_=w[g * K_PASS : (g + 1) * K_PASS, col0 : col0 + CHUNK].rearrange(
+                out=raw[:, :, :cols],
+                in_=w[g * K_PASS : (g + 1) * K_PASS, col0 : col0 + cols].rearrange(
                     "(t p) w -> p t w", p=P
                 ),
             )
             return raw
 
-        def regroup_chunk(raw):
+        def regroup(raw, first, cols, vector_cols):
             grouped = stream.tile([P, CHUNK, PACK], BF16, bufs=GROUPED_BUFS, align_bytes=64)
-            turned = psum_w.tile([P, TENSOR_COLS, PACK], BF16, tag="turned")
-            for c0 in range(0, TENSOR_COLS, P):
-                nc.tensor.matmul(
-                    turned[:, c0 : c0 + P, :],
-                    ident[:],
-                    raw[:, :, c0 : c0 + P].rearrange("p t c -> p c t"),
-                    start=True,
-                    stop=True,
-                )
-            first_v = CHUNK - VECTOR_COLS
-            for copy, first, end in (
-                (nc.vector.tensor_copy, first_v, CHUNK),
-                (nc.scalar.copy, TENSOR_COLS, first_v),
-            ):
+            split = cols - vector_cols * cols // CHUNK
+            for copy, a, b in ((nc.vector.tensor_copy, split, cols), (nc.scalar.copy, 0, split)):
                 copy(
-                    out=grouped[:, first:end, :].rearrange("p (c i) t -> p c t i", i=RUN),
-                    in_=raw[:, :, first:end].rearrange("p t (c i) -> p c t i", i=RUN),
+                    out=grouped[:, a:b, :].rearrange("p (c i) t -> p c t i", i=RUN),
+                    in_=raw[:, :, first + a : first + b].rearrange("p t (c i) -> p c t i", i=RUN),
                 )
-            nc.scalar.copy(out=grouped[:, :TENSOR_COLS, :], in_=turned[:])
             return grouped
 
         def quantise_chunk(grouped, codes, scales):
             nc.vector.quantize_mx(
                 out=codes.bitcast(FP8X4),
                 scales=scales,
-                in_=grouped[:].rearrange("p w t -> p (w t)"),
+                in_=grouped[:, : codes.shape[1], :].rearrange("p w t -> p (w t)"),
             )
 
-        chunks = (
-            [(lin1_W1, 0, 0)]
-            + [(lin1_W0, g, c) for c in range(0, LIN_S, CHUNK) for g in range(in_passes)]
-            + [(lin2_W0, h, HID_S) for h in range(s_passes)]
-            + [(lin2_W1, h, 0) for h in range(v_passes)]
-            + [(lin2_W0, h, c) for c in range(0, HID_S, CHUNK) for h in range(s_passes)]
-        )
+        loads = []
+        parts = []
+
+        def add_chunks(w, passes, col0, vector_cols, in_parts=1):
+            loads.extend([(w, g, col0, CHUNK) for g in range(passes)])
+            n = CHUNK // in_parts
+            for j in range(in_parts):
+                for g in range(passes):
+                    parts.append((len(loads) - passes + g, j * n, n, vector_cols))
+
+        add_chunks(lin1_W1, 1, 0, VECTOR_COLS_EARLY)
+        add_chunks(lin1_W0, in_passes, HID_S, VECTOR_COLS_EARLY)
+        for col0 in range(0, HID_S, CHUNK):
+            add_chunks(lin1_W0, in_passes, col0, VECTOR_COLS)
+        add_chunks(lin2_W0, s_passes, HID_S, VECTOR_COLS)
+        add_chunks(lin2_W1, v_passes, 0, VECTOR_COLS)
+        add_chunks(lin2_W0, s_passes, 0, VECTOR_COLS)
+        add_chunks(lin2_W0, s_passes, CHUNK, VECTOR_COLS, LAST_PARTS)
+        last = CHUNK // LAST_PARTS
         raws = []
         regrouped = []
         quantised = []
 
         def load_until(n):
-            while len(raws) < min(n, len(chunks)):
-                raws.append(load_chunk(*chunks[len(raws)]))
+            while len(raws) < min(n, len(loads)):
+                raws.append(load(*loads[len(raws)]))
 
         def regroup_until(n):
-            while len(regrouped) < min(n, len(chunks)):
-                load_until(len(regrouped) + 1)
-                regrouped.append(regroup_chunk(raws[len(regrouped)]))
+            while len(regrouped) < min(n, len(parts)):
+                i, c, cols, vector_cols = parts[len(regrouped)]
+                load_until(i + 1)
+                regrouped.append(regroup(raws[i], c, cols, vector_cols))
 
-        def next_weight_chunk(codes, scales):
+        def next_weights(codes, scales):
             i = len(quantised)
-            load_until(i + 1 + LOAD_AHEAD)
-            regroup_until(i + 2)
+            load_until(parts[i][0] + 1 + LOAD_AHEAD)
+            regroup_until(i + 1 + REGROUP_AHEAD)
             quantise_chunk(regrouped[i], codes, scales)
             quantised.append(i)
 
@@ -155,6 +156,8 @@ def tile_feedforward_pa_kernel(tc, features, lin1_W0, lin1_W1, lin2_W0, lin2_W1,
             regroup_until(1)
 
             with tc.tile_pool(name="flip", bufs=1) as flip:
+                ident = flip.tile([P, P], BF16)
+                make_identity(nc, ident[:])
                 xs_grouped = flip.tile([P, in_passes, NODES, PACK], BF16, align_bytes=64)
                 xv_grouped = flip.tile([P, DV, NODES, PACK], BF16, align_bytes=64)
                 for nt in range(NODE_TILES):
@@ -166,7 +169,7 @@ def tile_feedforward_pa_kernel(tc, features, lin1_W0, lin1_W1, lin2_W0, lin2_W1,
                         for t in range(PACK):
                             k0 = g * K_PASS + t * P
                             nc.tensor.transpose(flipped[:, t, :], x_rows[:, k0 : k0 + P], ident[:])
-                        nc.vector.tensor_copy(
+                        nc.scalar.copy(
                             out=xs_grouped[:, g, nodes, :],
                             in_=flipped[:].rearrange("p t n -> p n t"),
                         )
@@ -192,13 +195,12 @@ def tile_feedforward_pa_kernel(tc, features, lin1_W0, lin1_W1, lin2_W0, lin2_W1,
                         scales=xv_scales[:, d, :],
                         in_=xv_grouped[:, d, :, :].rearrange("p n t -> p (n t)"),
                     )
-
-            next_weight_chunk(w11_codes[:], w11_scales[:])
+            next_weights(w11_codes[:], w11_scales[:])
 
             def layer1_weights(col0):
                 for g in range(in_passes):
                     cols = slice(col0, col0 + CHUNK)
-                    next_weight_chunk(w10_codes[:, g, cols], w10_scales[:, g, cols])
+                    next_weights(w10_codes[:, g, cols], w10_scales[:, g, cols])
 
             def layer1_scalars(channel0, nt):
                 nodes = slice(nt * P, (nt + 1) * P)
@@ -218,47 +220,58 @@ def tile_feedforward_pa_kernel(tc, features, lin1_W0, lin1_W1, lin2_W0, lin2_W1,
                 return bank
 
             with tc.tile_pool(name="hidden", bufs=3) as hidden:
-                for col0 in range(0, HID_S, CHUNK):
-                    layer1_weights(col0)
-                    for h in range(col0 // K_PASS, (col0 + CHUNK) // K_PASS):
-                        s_grouped = hidden.tile([P, NODES, PACK], BF16, align_bytes=64)
-                        for nt in range(NODE_TILES):
-                            bank = layer1_scalars(h * K_PASS, nt)
-                            nc.scalar.activation(
-                                out=s_grouped[:, nt * P : (nt + 1) * P, :],
-                                in_=bank[:].rearrange("p t n -> p n t"),
-                                func=ACT.Silu,
-                                scale=1.0 / math.sqrt(IN_S),
-                            )
-                        nc.vector.quantize_mx(
-                            out=g1s_codes[:, h, :].bitcast(FP8X4),
-                            scales=g1s_scales[:, h, :],
-                            in_=s_grouped[:].rearrange("p n t -> p (n t)"),
-                        )
-
                 gate1 = hidden.tile([P, v_passes, NODES, PACK], F32, bufs=1)
-                layer1_weights(HID_S)
-                for h in range(v_passes):
-                    for nt in range(NODE_TILES):
-                        bank = layer1_scalars(HID_S + h * K_PASS, nt)
-                        nc.scalar.activation(
-                            out=gate1[:, h, nt * P : (nt + 1) * P, :],
-                            in_=bank[:].rearrange("p t n -> p n t"),
-                            func=ACT.Tanh,
-                            scale=0.5 / math.sqrt(IN_S),
-                        )
-                    gate_h = gate1[:, h, :, :].rearrange("p n t -> p (n t)")
-                    nc.vector.tensor_scalar(
-                        out=gate_h,
-                        in0=gate_h,
-                        scalar1=0.5 / math.sqrt(IN_V),
-                        scalar2=0.5 / math.sqrt(IN_V),
-                        op0=ALU.mult,
-                        op1=ALU.add,
-                    )
 
-                for h in range(v_passes):
-                    for d in range(DV):
+                def layer1_silu():
+                    for col0 in range(0, HID_S, CHUNK):
+                        layer1_weights(col0)
+                        for h in range(col0 // K_PASS, (col0 + CHUNK) // K_PASS):
+                            s_grouped = hidden.tile([P, NODES, PACK], BF16, align_bytes=64)
+                            for nt in range(NODE_TILES):
+                                bank = layer1_scalars(h * K_PASS, nt)
+                                nc.scalar.activation(
+                                    out=s_grouped[:, nt * P : (nt + 1) * P, :],
+                                    in_=bank[:].rearrange("p t n -> p n t"),
+                                    func=ACT.Silu,
+                                    scale=1.0 / math.sqrt(IN_S),
+                                )
+                            nc.vector.quantize_mx(
+                                out=g1s_codes[:, h, :].bitcast(FP8X4),
+                                scales=g1s_scales[:, h, :],
+                                in_=s_grouped[:].rearrange("p n t -> p (n t)"),
+                            )
+
+                def layer1_gates():
+                    layer1_weights(HID_S)
+                    for h in range(v_passes):
+                        for nt in range(NODE_TILES):
+                            bank = layer1_scalars(HID_S + h * K_PASS, nt)
+                            nc.scalar.activation(
+                                out=gate1[:, h, nt * P : (nt + 1) * P, :],
+                                in_=bank[:].rearrange("p t n -> p n t"),
+                                func=ACT.Tanh,
+                                scale=0.5 / math.sqrt(IN_S),
+                            )
+                        gate_h = gate1[:, h, :, :].rearrange("p n t -> p (n t)")
+                        nc.vector.tensor_scalar(
+                            out=gate_h,
+                            in0=gate_h,
+                            scalar1=0.5 / math.sqrt(IN_V),
+                            scalar2=0.5 / math.sqrt(IN_V),
+                            op0=ALU.mult,
+                            op1=ALU.add,
+                        )
+
+                def layer1_vectors():
+                    def quantise_v(h, d, v_grouped):
+                        nc.vector.quantize_mx(
+                            out=g1v_codes[:, h, d, :].bitcast(FP8X4),
+                            scales=g1v_scales[:, h, d, :],
+                            in_=v_grouped[:].rearrange("p n t -> p (n t)"),
+                        )
+
+                    waiting = []
+                    for h, d in [(h, d) for h in range(v_passes) for d in range(DV)]:
                         v_grouped = hidden.tile([P, NODES, PACK], BF16, align_bytes=64)
                         for nt in range(NODE_TILES):
                             nodes = slice(nt * P, (nt + 1) * P)
@@ -280,22 +293,25 @@ def tile_feedforward_pa_kernel(tc, features, lin1_W0, lin1_W1, lin2_W0, lin2_W1,
                                 in1=gate1[:, h, nodes, :],
                                 op=ALU.mult,
                             )
-                        nc.vector.quantize_mx(
-                            out=g1v_codes[:, h, d, :].bitcast(FP8X4),
-                            scales=g1v_scales[:, h, d, :],
-                            in_=v_grouped[:].rearrange("p n t -> p (n t)"),
-                        )
+                            if nt == 0 and waiting:
+                                quantise_v(*waiting.pop())
+                        waiting.append((h, d, v_grouped))
+                    quantise_v(*waiting.pop())
 
-        def layer2_scalars():
+                layer1_gates()
+                layer1_vectors()
+                layer1_silu()
+
+        def layer2_scalars(cols_n):
             banks = [
-                [psum_s.tile([P, BANK], F32, name="acc", tag="bank") for j in range(CHUNK // BANK)]
+                [psum_s.tile([P, BANK], F32, name="acc", tag="bank") for j in range(cols_n // BANK)]
                 for nt in range(NODE_TILES)
             ]
             for h in range(s_passes):
-                w20_codes = stream.tile([P, CHUNK], U32, bufs=12, align_bytes=64)
-                w20_scales = stream.tile([P, CHUNK], U8, bufs=12, align_bytes=64)
-                next_weight_chunk(w20_codes[:], w20_scales[:])
-                for j in range(CHUNK // BANK):
+                w20_codes = stream.tile([P, CHUNK], U32, bufs=W20_BUFS, align_bytes=64)
+                w20_scales = stream.tile([P, CHUNK], U8, bufs=W20_BUFS, align_bytes=64)
+                next_weights(w20_codes[:, :cols_n], w20_scales[:, :cols_n])
+                for j in range(cols_n // BANK):
                     cols = slice(j * BANK, (j + 1) * BANK)
                     for nt in range(NODE_TILES):
                         nodes = slice(nt * P, (nt + 1) * P)
@@ -310,7 +326,7 @@ def tile_feedforward_pa_kernel(tc, features, lin1_W0, lin1_W1, lin2_W0, lin2_W1,
                         )
             return banks
 
-        banks = layer2_scalars()
+        banks = layer2_scalars(CHUNK)
         for nt in range(NODE_TILES):
             for j in range(CHUNK // BANK):
                 nc.scalar.activation(
@@ -359,13 +375,8 @@ def tile_feedforward_pa_kernel(tc, features, lin1_W0, lin1_W1, lin2_W0, lin2_W1,
                         in_=v_out[:].rearrange("p o d -> p (o d)"),
                     )
 
-            for h in range(v_passes):
-                next_weight_chunk(w21_codes[:, h, :], w21_scales[:, h, :])
-            layer2_vectors(0)
-
-            for col0 in range(0, HID_S, CHUNK):
-                banks = layer2_scalars()
-                for j in range(CHUNK // BANK):
+            def silu_out(banks, col0, n):
+                for j in range(n // BANK):
                     for nt in range(NODE_TILES):
                         s_out = layer2.tile([P, BANK], F32)
                         nc.scalar.activation(
@@ -379,4 +390,10 @@ def tile_feedforward_pa_kernel(tc, features, lin1_W0, lin1_W1, lin2_W0, lin2_W1,
                             in_=s_out[:],
                         )
 
+            for h in range(v_passes):
+                next_weights(w21_codes[:, h, :], w21_scales[:, h, :])
+            layer2_vectors(0)
+            silu_out(layer2_scalars(CHUNK), 0, CHUNK)
             layer2_vectors(1)
+            for j in range(LAST_PARTS):
+                silu_out(layer2_scalars(last), CHUNK + j * last, last)

@@ -29,7 +29,7 @@ CHUNK = 1024
 VECTOR_COLS_EARLY = 640
 VECTOR_COLS = 448
 LAST_PARTS = 2
-RUN = 4
+RUN = 2
 V_STORE = 256
 RAW_BUFS = 7
 LOAD_AHEAD = 6

@@ -26,14 +26,20 @@ HID_V = 1024
 LIN_S = HID_S + HID_V
 
 CHUNK = 1024
-VECTOR_COLS_EARLY = 640
-VECTOR_COLS = 448
+EARLY_SHARES = (0, 704)
+LAYER1_SHARES = (0, 448)
+LAYER2_SHARES = (256, 384)
+TURN_COLS = 256
 LAST_PARTS = 2
 RUN = 2
 V_STORE = 256
 RAW_BUFS = 7
 LOAD_AHEAD = 6
 REGROUP_AHEAD = 2
+TURN_AHEAD = 1
+UNITS_E = 2
+UNITS_F = 1
+UNIT_LEAD = 2
 GROUPED_BUFS = 5
 W20_BUFS = 6
 
@@ -49,8 +55,11 @@ def tile_feedforward_pa_kernel(tc, features, lin1_W0, lin1_W1, lin2_W0, lin2_W1,
     with tc.tile_pool(name="keep", bufs=1) as keep, tc.tile_pool(
         name="stream", bufs=1
     ) as stream, tc.psum_pool(name="psum_s", bufs=4) as psum_s, tc.psum_pool(
-        name="psum_v", bufs=4
-    ) as psum_v:
+        name="psum_v", bufs=2
+    ) as psum_v, tc.psum_pool(name="psum_w", bufs=2) as psum_w:
+
+        ident = keep.tile([P, P], BF16)
+        make_identity(nc, ident[:])
 
         def load(w, g, col0, cols):
             raw = stream.tile([P, PACK, CHUNK], BF16, bufs=RAW_BUFS)
@@ -62,14 +71,33 @@ def tile_feedforward_pa_kernel(tc, features, lin1_W0, lin1_W1, lin2_W0, lin2_W1,
             )
             return raw
 
-        def regroup(raw, first, cols, vector_cols):
+        def turn(raw, first, cols, shares):
+            tensor_cols = shares[0] * cols // CHUNK
+            if not tensor_cols:
+                return None
+            turned = psum_w.tile([P, TURN_COLS, PACK], BF16, tag="turned")
+            for c0 in range(0, tensor_cols, P):
+                nc.tensor.matmul(
+                    turned[:, c0 : c0 + P, :].rearrange("p c t -> p t c"),
+                    ident[:],
+                    raw[:, :, first + c0 : first + c0 + P],
+                    start=True,
+                    stop=True,
+                )
+            return turned
+
+        def regroup(raw, turned, first, cols, shares):
             grouped = stream.tile([P, CHUNK, PACK], BF16, bufs=GROUPED_BUFS, align_bytes=64)
+            tensor_cols, vector_cols = shares
+            tensor_cols = tensor_cols * cols // CHUNK
             split = cols - vector_cols * cols // CHUNK
-            for copy, a, b in ((nc.vector.tensor_copy, split, cols), (nc.scalar.copy, 0, split)):
+            for copy, a, b in ((nc.vector.tensor_copy, split, cols), (nc.scalar.copy, tensor_cols, split)):
                 copy(
                     out=grouped[:, a:b, :].rearrange("p (c i) t -> p c t i", i=RUN),
                     in_=raw[:, :, first + a : first + b].rearrange("p t (c i) -> p c t i", i=RUN),
                 )
+            if tensor_cols:
+                nc.scalar.copy(out=grouped[:, :tensor_cols, :], in_=turned[:, :tensor_cols, :])
             return grouped
 
         def quantise_chunk(grouped, codes, scales):
@@ -89,16 +117,17 @@ def tile_feedforward_pa_kernel(tc, features, lin1_W0, lin1_W1, lin2_W0, lin2_W1,
                 for g in range(passes):
                     parts.append((len(loads) - passes + g, j * n, n, vector_cols))
 
-        add_chunks(lin1_W1, 1, 0, VECTOR_COLS_EARLY)
-        add_chunks(lin1_W0, in_passes, HID_S, VECTOR_COLS_EARLY)
+        add_chunks(lin1_W1, 1, 0, EARLY_SHARES)
+        add_chunks(lin1_W0, in_passes, HID_S, EARLY_SHARES)
         for col0 in range(0, HID_S, CHUNK):
-            add_chunks(lin1_W0, in_passes, col0, VECTOR_COLS)
-        add_chunks(lin2_W0, s_passes, HID_S, VECTOR_COLS)
-        add_chunks(lin2_W1, v_passes, 0, VECTOR_COLS)
-        add_chunks(lin2_W0, s_passes, 0, VECTOR_COLS)
-        add_chunks(lin2_W0, s_passes, CHUNK, VECTOR_COLS, LAST_PARTS)
+            add_chunks(lin1_W0, in_passes, col0, LAYER1_SHARES)
+        add_chunks(lin2_W0, s_passes, HID_S, LAYER2_SHARES)
+        add_chunks(lin2_W1, v_passes, 0, LAYER2_SHARES)
+        add_chunks(lin2_W0, s_passes, 0, LAYER2_SHARES)
+        add_chunks(lin2_W0, s_passes, CHUNK, LAYER2_SHARES, LAST_PARTS)
         last = CHUNK // LAST_PARTS
         raws = []
+        turned_parts = []
         regrouped = []
         quantised = []
 
@@ -106,15 +135,23 @@ def tile_feedforward_pa_kernel(tc, features, lin1_W0, lin1_W1, lin2_W0, lin2_W1,
             while len(raws) < min(n, len(loads)):
                 raws.append(load(*loads[len(raws)]))
 
+        def turn_until(n):
+            while len(turned_parts) < min(n, len(parts)):
+                i, c, cols, shares = parts[len(turned_parts)]
+                load_until(i + 1)
+                turned_parts.append(turn(raws[i], c, cols, shares))
+
         def regroup_until(n):
             while len(regrouped) < min(n, len(parts)):
-                i, c, cols, vector_cols = parts[len(regrouped)]
-                load_until(i + 1)
-                regrouped.append(regroup(raws[i], c, cols, vector_cols))
+                k = len(regrouped)
+                i, c, cols, shares = parts[k]
+                turn_until(k + 1)
+                regrouped.append(regroup(raws[i], turned_parts[k], c, cols, shares))
 
         def next_weights(codes, scales):
             i = len(quantised)
             load_until(parts[i][0] + 1 + LOAD_AHEAD)
+            turn_until(i + 1 + REGROUP_AHEAD + TURN_AHEAD)
             regroup_until(i + 1 + REGROUP_AHEAD)
             quantise_chunk(regrouped[i], codes, scales)
             quantised.append(i)
@@ -156,8 +193,6 @@ def tile_feedforward_pa_kernel(tc, features, lin1_W0, lin1_W1, lin2_W0, lin2_W1,
             regroup_until(1)
 
             with tc.tile_pool(name="flip", bufs=1) as flip:
-                ident = flip.tile([P, P], BF16)
-                make_identity(nc, ident[:])
                 xs_grouped = flip.tile([P, in_passes, NODES, PACK], BF16, align_bytes=64)
                 xv_grouped = flip.tile([P, DV, NODES, PACK], BF16, align_bytes=64)
                 for nt in range(NODE_TILES):
@@ -175,7 +210,7 @@ def tile_feedforward_pa_kernel(tc, features, lin1_W0, lin1_W1, lin2_W0, lin2_W1,
                         )
                     x_vec = x_rows[:, IN_S:].rearrange("n (i d) -> n d i", d=DV)
                     for d in range(DV):
-                        flipped = psum_v.tile([P, PACK, P], BF16, tag="bank")
+                        flipped = psum_s.tile([P, PACK, P], BF16, tag="bank")
                         for t in range(PACK):
                             nc.tensor.transpose(
                                 flipped[:, t, :], x_vec[:, d, t * P : (t + 1) * P], ident[:]
@@ -299,10 +334,23 @@ def tile_feedforward_pa_kernel(tc, features, lin1_W0, lin1_W1, lin2_W0, lin2_W1,
                     quantise_v(*waiting.pop())
 
                 layer1_gates()
-                layer1_vectors()
                 layer1_silu()
+                layer1_vectors()
 
-        def layer2_scalars(cols_n):
+        units = []
+        begun = []
+
+        def side(n):
+            for j in range(n + 1):
+                while units and len(begun) < UNIT_LEAD:
+                    tensor_part, evacuate = units.pop(0)
+                    begun.append((evacuate, tensor_part()))
+                if j < n and begun:
+                    evacuate, got = begun.pop(0)
+                    evacuate(got)
+
+        def layer2_scalars(cols_n, n_side, acts=()):
+            acts = list(acts)
             banks = [
                 [psum_s.tile([P, BANK], F32, name="acc", tag="bank") for j in range(cols_n // BANK)]
                 for nt in range(NODE_TILES)
@@ -311,6 +359,9 @@ def tile_feedforward_pa_kernel(tc, features, lin1_W0, lin1_W1, lin2_W0, lin2_W1,
                 w20_codes = stream.tile([P, CHUNK], U32, bufs=W20_BUFS, align_bytes=64)
                 w20_scales = stream.tile([P, CHUNK], U8, bufs=W20_BUFS, align_bytes=64)
                 next_weights(w20_codes[:, :cols_n], w20_scales[:, :cols_n])
+                if h == 0:
+                    for act in acts:
+                        act()
                 for j in range(cols_n // BANK):
                     cols = slice(j * BANK, (j + 1) * BANK)
                     for nt in range(NODE_TILES):
@@ -324,76 +375,103 @@ def tile_feedforward_pa_kernel(tc, features, lin1_W0, lin1_W1, lin2_W0, lin2_W1,
                             start=(h == 0),
                             stop=(h == s_passes - 1),
                         )
+                side(n_side)
             return banks
 
-        banks = layer2_scalars(CHUNK)
-        for nt in range(NODE_TILES):
-            for j in range(CHUNK // BANK):
-                nc.scalar.activation(
-                    out=gate2[:, nt, j * BANK : (j + 1) * BANK],
-                    in_=banks[nt][j][:],
-                    func=ACT.Tanh,
-                    scale=0.5 / math.sqrt(HID_S),
-                )
-            nc.vector.tensor_scalar(
-                out=gate2[:, nt, :],
-                in0=gate2[:, nt, :],
-                scalar1=0.5 / math.sqrt(HID_V),
-                scalar2=0.5 / math.sqrt(HID_V),
-                op0=ALU.mult,
-                op1=ALU.add,
-            )
+        compute = {mybir.EngineType.PE, mybir.EngineType.DVE, mybir.EngineType.Activation}
+        with tc.tile_pool(name="layer2", bufs=8) as layer2, tc.manual_schedule(engines=compute):
+            banks = layer2_scalars(CHUNK, 0)
 
-        with tc.tile_pool(name="layer2", bufs=8) as layer2:
-
-            def layer2_vectors(nt):
-                nodes = slice(nt * P, (nt + 1) * P)
-                for c0 in range(0, HID_V, V_STORE):
-                    v_out = layer2.tile([P, V_STORE, DV], F32, bufs=4)
-                    for c1 in range(0, V_STORE, P):
-                        chans = slice(c0 + c1, c0 + c1 + P)
-                        bank = psum_v.tile([P, DV, P], F32, tag="bank")
-                        for d in range(DV):
-                            for h in range(v_passes):
-                                mx(
-                                    bank[:, d, :],
-                                    g1v_codes[:, h, d, nodes],
-                                    g1v_scales[:, h, d, nodes],
-                                    w21_codes[:, h, chans],
-                                    w21_scales[:, h, chans],
-                                    start=(h == 0),
-                                    stop=(h == v_passes - 1),
-                                )
-                        nc.vector.tensor_tensor(
-                            out=v_out[:, c1 : c1 + P, :],
-                            in0=bank[:].rearrange("p d o -> p o d"),
-                            in1=gate2[:, nt, chans].unsqueeze(2).to_broadcast([P, P, DV]),
-                            op=ALU.mult,
+            def gates2(banks):
+                for nt in range(NODE_TILES):
+                    for j in range(CHUNK // BANK):
+                        nc.scalar.activation(
+                            out=gate2[:, nt, j * BANK : (j + 1) * BANK],
+                            in_=banks[nt][j][:],
+                            func=ACT.Tanh,
+                            scale=0.5 / math.sqrt(HID_S),
                         )
-                    nc.sync.dma_start(
-                        out=out[nodes, HID_S + DV * c0 : HID_S + DV * (c0 + V_STORE)],
-                        in_=v_out[:].rearrange("p o d -> p (o d)"),
+
+            def rescale2():
+                for nt in range(NODE_TILES):
+                    nc.vector.tensor_scalar(
+                        out=gate2[:, nt, :],
+                        in0=gate2[:, nt, :],
+                        scalar1=0.5 / math.sqrt(HID_V),
+                        scalar2=0.5 / math.sqrt(HID_V),
+                        op0=ALU.mult,
+                        op1=ALU.add,
                     )
 
-            def silu_out(banks, col0, n):
-                for j in range(n // BANK):
-                    for nt in range(NODE_TILES):
-                        s_out = layer2.tile([P, BANK], F32)
-                        nc.scalar.activation(
-                            out=s_out[:],
-                            in_=banks[nt][j][:],
-                            func=ACT.Silu,
-                            scale=1.0 / math.sqrt(HID_S),
-                        )
+            outs = {}
+
+            def out_unit(nt, c):
+                nodes = slice(nt * P, (nt + 1) * P)
+                chans = slice(c * P, (c + 1) * P)
+                per = V_STORE // P
+
+                def tensor_part():
+                    bank = psum_v.tile([P, DV, P], F32, tag="bank")
+                    for d in range(DV):
+                        for h in range(v_passes):
+                            mx(
+                                bank[:, d, :],
+                                g1v_codes[:, h, d, nodes],
+                                g1v_scales[:, h, d, nodes],
+                                w21_codes[:, h, chans],
+                                w21_scales[:, h, chans],
+                                start=(h == 0),
+                                stop=(h == v_passes - 1),
+                            )
+                    return bank
+
+                def evacuate(bank):
+                    if c % per == 0:
+                        v_out = layer2.tile([P, V_STORE, DV], F32, bufs=4)
+                        outs[nt, c // per] = v_out
+                    v_out = outs[nt, c // per]
+                    nc.vector.tensor_tensor(
+                        out=v_out[:, (c % per) * P : (c % per + 1) * P, :],
+                        in0=bank[:].rearrange("p d o -> p o d"),
+                        in1=gate2[:, nt, chans].unsqueeze(2).to_broadcast([P, P, DV]),
+                        op=ALU.mult,
+                    )
+                    if c % per == per - 1:
+                        c0 = (c // per) * V_STORE
                         nc.sync.dma_start(
-                            out=out[nt * P : (nt + 1) * P, col0 + j * BANK : col0 + (j + 1) * BANK],
-                            in_=s_out[:],
+                            out=out[nodes, HID_S + DV * c0 : HID_S + DV * (c0 + V_STORE)],
+                            in_=v_out[:].rearrange("p o d -> p (o d)"),
                         )
 
-            for h in range(v_passes):
-                next_weights(w21_codes[:, h, :], w21_scales[:, h, :])
-            layer2_vectors(0)
-            silu_out(layer2_scalars(CHUNK), 0, CHUNK)
-            layer2_vectors(1)
+                return tensor_part, evacuate
+
+            def silu_acts(banks, col0, n):
+                return [lambda j=j, nt=nt: silu_out(banks, col0, j, nt) for j in range(n // BANK) for nt in range(NODE_TILES)]
+
+            def silu_out(banks, col0, j, nt):
+                s_out = layer2.tile([P, BANK], F32)
+                nc.scalar.activation(
+                    out=s_out[:],
+                    in_=banks[nt][j][:],
+                    func=ACT.Silu,
+                    scale=1.0 / math.sqrt(HID_S),
+                )
+                nc.sync.dma_start(
+                    out=out[nt * P : (nt + 1) * P, col0 + j * BANK : col0 + (j + 1) * BANK],
+                    in_=s_out[:],
+                )
+
+            next_weights(w21_codes[:, 0, :], w21_scales[:, 0, :])
+            gates2(banks)
+            next_weights(w21_codes[:, 1, :], w21_scales[:, 1, :])
+            rescale2()
+            units.extend([out_unit(nt, c) for nt in range(NODE_TILES) for c in range(HID_V // P)])
+            side(0)
+            banks = layer2_scalars(CHUNK, UNITS_E)
+            acts = silu_acts(banks, 0, CHUNK)
             for j in range(LAST_PARTS):
-                silu_out(layer2_scalars(last), CHUNK + j * last, last)
+                banks = layer2_scalars(last, UNITS_F, acts)
+                acts = silu_acts(banks, CHUNK + j * last, last)
+            for act in acts:
+                act()
+            side(len(units) + len(begun))

@@ -31,6 +31,7 @@ LAYER1_SHARES = (0, 448)
 LAYER2_SHARES = (256, 384)
 TURN_COLS = 256
 LAST_PARTS = 2
+ROW_PAD = 32
 RUN = 2
 V_STORE = 256
 RAW_BUFS = 7
@@ -62,7 +63,7 @@ def tile_feedforward_pa_kernel(tc, features, lin1_W0, lin1_W1, lin2_W0, lin2_W1,
         make_identity(nc, ident[:])
 
         def load(w, g, col0, cols):
-            raw = stream.tile([P, PACK, CHUNK], BF16, bufs=RAW_BUFS)
+            raw = stream.tile([P, PACK, CHUNK + ROW_PAD], BF16, bufs=RAW_BUFS)
             nc.sync.dma_start(
                 out=raw[:, :, :cols],
                 in_=w[g * K_PASS : (g + 1) * K_PASS, col0 : col0 + cols].rearrange(

import math

import concourse.mybir as mybir
from concourse.masks import make_identity

BF16 = mybir.dt.bfloat16
F32 = mybir.dt.float32
U32 = mybir.dt.uint32
U8 = mybir.dt.uint8
FP8X4 = mybir.dt.float8_e4m3fn_x4
ACT = mybir.ActivationFunctionType
ALU = mybir.AluOpType

P = 128
PACK = 4
K_PASS = P * PACK
BANK = 512

NODES = 256
NODE_TILES = NODES // P
DV = 3
IN_S = 1024
IN_V = 512
HID_S = 2048
HID_V = 1024
LIN_S = HID_S + HID_V

CHUNK = 1024
EARLY_SHARES = (0, 704)
LAYER1_SHARES = (0, 448)
LAYER2_SHARES = (256, 384)
TURN_COLS = 256
LAST_PARTS = 2
ROW_PAD = 32
RUN = 2
V_STORE = 256
RAW_BUFS = 7
LOAD_AHEAD = 6
REGROUP_AHEAD = 2
TURN_AHEAD = 1
UNITS_E = 2
UNITS_F = 1
UNIT_LEAD = 2
GROUPED_BUFS = 5
W20_BUFS = 6

FLOPS = 2 * NODES * (IN_S + HID_S) * LIN_S + 2 * NODES * DV * (IN_V + HID_V) * HID_V


def tile_feedforward_pa_kernel(tc, features, lin1_W0, lin1_W1, lin2_W0, lin2_W1, out):
    nc = tc.nc
    in_passes = IN_S // K_PASS
    s_passes = HID_S // K_PASS
    v_passes = HID_V // K_PASS

    with tc.tile_pool(name="keep", bufs=1) as keep, tc.tile_pool(
        name="stream", bufs=1
    ) as stream, tc.psum_pool(name="psum_s", bufs=4) as psum_s, tc.psum_pool(
        name="psum_v", bufs=2
    ) as psum_v, tc.psum_pool(name="psum_w", bufs=2) as psum_w:

        ident = keep.tile([P, P], BF16)
        make_identity(nc, ident[:])

        def load(w, g, col0, cols):
            raw = stream.tile([P, PACK, CHUNK + ROW_PAD], BF16, bufs=RAW_BUFS)
            nc.sync.dma_start(
                out=raw[:, :, :cols],
                in_=w[g * K_PASS : (g + 1) * K_PASS, col0 : col0 + cols].rearrange(
                    "(t p) w -> p t w", p=P
                ),
            )
            return raw

        def turn(raw, first, cols, shares):
            tensor_cols = shares[0] * cols // CHUNK
            if not tensor_cols:
                return None
            turned = psum_w.tile([P, TURN_COLS, PACK], BF16, tag="turned")
            for c0 in range(0, tensor_cols, P):
                nc.tensor.matmul(
                    turned[:, c0 : c0 + P, :].rearrange("p c t -> p t c"),
                    ident[:],
                    raw[:, :, first + c0 : first + c0 + P],
                    start=True,
                    stop=True,
                )
            return turned

        def regroup(raw, turned, first, cols, shares):
            grouped = stream.tile([P, CHUNK, PACK], BF16, bufs=GROUPED_BUFS, align_bytes=64)
            tensor_cols, vector_cols = shares
            tensor_cols = tensor_cols * cols // CHUNK
            split = cols - vector_cols * cols // CHUNK
            for copy, a, b in ((nc.vector.tensor_copy, split, cols), (nc.scalar.copy, tensor_cols, split)):
                copy(
                    out=grouped[:, a:b, :].rearrange("p (c i) t -> p c t i", i=RUN),
                    in_=raw[:, :, first + a : first + b].rearrange("p t (c i) -> p c t i", i=RUN),
                )
            if tensor_cols:
                nc.scalar.copy(out=grouped[:, :tensor_cols, :], in_=turned[:, :tensor_cols, :])
            return grouped

        def quantise_chunk(grouped, codes, scales):
            nc.vector.quantize_mx(
                out=codes.bitcast(FP8X4),
                scales=scales,
                in_=grouped[:, : codes.shape[1], :].rearrange("p w t -> p (w t)"),
            )

        loads = []
        parts = []

        def add_chunks(w, passes, col0, vector_cols, in_parts=1):
            loads.extend([(w, g, col0, CHUNK) for g in range(passes)])
            n = CHUNK // in_parts
            for j in range(in_parts):
                for g in range(passes):
                    parts.append((len(loads) - passes + g, j * n, n, vector_cols))

        add_chunks(lin1_W1, 1, 0, EARLY_SHARES)
        add_chunks(lin1_W0, in_passes, HID_S, EARLY_SHARES)
        for col0 in range(0, HID_S, CHUNK):
            add_chunks(lin1_W0, in_passes, col0, LAYER1_SHARES)
        add_chunks(lin2_W0, s_passes, HID_S, LAYER2_SHARES)
        add_chunks(lin2_W1, v_passes, 0, LAYER2_SHARES)
        add_chunks(lin2_W0, s_passes, 0, LAYER2_SHARES)
        add_chunks(lin2_W0, s_passes, CHUNK, LAYER2_SHARES, LAST_PARTS)
        last = CHUNK // LAST_PARTS
        raws = []
        turned_parts = []
        regrouped = []
        quantised = []

        def load_until(n):
            while len(raws) < min(n, len(loads)):
                raws.append(load(*loads[len(raws)]))

        def turn_until(n):
            while len(turned_parts) < min(n, len(parts)):
                i, c, cols, shares = parts[len(turned_parts)]
                load_until(i + 1)
                turned_parts.append(turn(raws[i], c, cols, shares))

        def regroup_until(n):
            while len(regrouped) < min(n, len(parts)):
                k = len(regrouped)
                i, c, cols, shares = parts[k]
                turn_until(k + 1)
                regrouped.append(regroup(raws[i], turned_parts[k], c, cols, shares))

        def next_weights(codes, scales):
            i = len(quantised)
            load_until(parts[i][0] + 1 + LOAD_AHEAD)
            turn_until(i + 1 + REGROUP_AHEAD + TURN_AHEAD)
            regroup_until(i + 1 + REGROUP_AHEAD)
            quantise_chunk(regrouped[i], codes, scales)
            quantised.append(i)

        def mx(acc, a_codes, a_scales, b_codes, b_scales, start, stop):
            nc.tensor.matmul_mx(
                out=acc,
                lhsT=a_codes.bitcast(FP8X4),
                lhsT_scale=a_scales,
                rhs=b_codes.bitcast(FP8X4),
                rhs_scale=b_scales,
                start=start,
                stop=stop,
            )

        g1s_codes = keep.tile([P, s_passes, NODES], U32, align_bytes=64)
        g1s_scales = keep.tile([P, s_passes, NODES], U8, align_bytes=64)
        g1v_codes = keep.tile([P, v_passes, DV, NODES], U32, align_bytes=64)
        g1v_scales = keep.tile([P, v_passes, DV, NODES], U8, align_bytes=64)
        w21_codes = keep.tile([P, v_passes, HID_V], U32, align_bytes=64)
        w21_scales = keep.tile([P, v_passes, HID_V], U8, align_bytes=64)
        gate2 = keep.tile([P, NODE_TILES, HID_V], F32)

        with tc.tile_pool(name="layer1", bufs=1) as layer1:
            w10_codes = layer1.tile([P, in_passes, LIN_S], U32, align_bytes=64)
            w10_scales = layer1.tile([P, in_passes, LIN_S], U8, align_bytes=64)
            w11_codes = layer1.tile([P, HID_V], U32, align_bytes=64)
            w11_scales = layer1.tile([P, HID_V], U8, align_bytes=64)
            xs_codes = layer1.tile([P, in_passes, NODES], U32, align_bytes=64)
            xs_scales = layer1.tile([P, in_passes, NODES], U8, align_bytes=64)
            xv_codes = layer1.tile([P, DV, NODES], U32, align_bytes=64)
            xv_scales = layer1.tile([P, DV, NODES], U8, align_bytes=64)

            warm = layer1.tile([P, 1], F32)
            nc.vector.memset(warm[:], 0.0)
            nc.scalar.activation(out=warm[:], in_=warm[:], func=ACT.Silu)

            load_until(1)
            regroup_until(1)

            with tc.tile_pool(name="flip", bufs=1) as flip:
                xs_grouped = flip.tile([P, in_passes, NODES, PACK], BF16, align_bytes=64)
                xv_grouped = flip.tile([P, DV, NODES, PACK], BF16, align_bytes=64)
                for nt in range(NODE_TILES):
                    nodes = slice(nt * P, (nt + 1) * P)
                    x_rows = flip.tile([P, IN_S + DV * IN_V], BF16, bufs=NODE_TILES)
                    nc.sync.dma_start(out=x_rows[:], in_=features[nodes, :])
                    for g in range(in_passes):
                        flipped = psum_s.tile([P, PACK, P], BF16, tag="bank")
                        for t in range(PACK):
                            k0 = g * K_PASS + t * P
                            nc.tensor.transpose(flipped[:, t, :], x_rows[:, k0 : k0 + P], ident[:])
                        nc.scalar.copy(
                            out=xs_grouped[:, g, nodes, :],
                            in_=flipped[:].rearrange("p t n -> p n t"),
                        )
                    x_vec = x_rows[:, IN_S:].rearrange("n (i d) -> n d i", d=DV)
                    for d in range(DV):
                        flipped = psum_s.tile([P, PACK, P], BF16, tag="bank")
                        for t in range(PACK):
                            nc.tensor.transpose(
                                flipped[:, t, :], x_vec[:, d, t * P : (t + 1) * P], ident[:]
                            )
                        nc.scalar.copy(
                            out=xv_grouped[:, d, nodes, :],
                            in_=flipped[:].rearrange("p t n -> p n t"),
                        )
                nc.vector.quantize_mx(
                    out=xs_codes[:].rearrange("p g n -> p (g n)").bitcast(FP8X4),
                    scales=xs_scales[:].rearrange("p g n -> p (g n)"),
                    in_=xs_grouped[:].rearrange("p g n t -> p (g n t)"),
                )
                for d in range(DV):
                    nc.vector.quantize_mx(
                        out=xv_codes[:, d, :].bitcast(FP8X4),
                        scales=xv_scales[:, d, :],
                        in_=xv_grouped[:, d, :, :].rearrange("p n t -> p (n t)"),
                    )
            next_weights(w11_codes[:], w11_scales[:])

            def layer1_weights(col0):
                for g in range(in_passes):
                    cols = slice(col0, col0 + CHUNK)
                    next_weights(w10_codes[:, g, cols], w10_scales[:, g, cols])

            def layer1_scalars(channel0, nt):
                nodes = slice(nt * P, (nt + 1) * P)
                bank = psum_s.tile([P, PACK, P], F32, tag="bank")
                for t in range(PACK):
                    chans = slice(channel0 + t * P, channel0 + (t + 1) * P)
                    for g in range(in_passes):
                        mx(
                            bank[:, t, :],
                            w10_codes[:, g, chans],
                            w10_scales[:, g, chans],
                            xs_codes[:, g, nodes],
                            xs_scales[:, g, nodes],
                            start=(g == 0),
                            stop=(g == in_passes - 1),
                        )
                return bank

            with tc.tile_pool(name="hidden", bufs=3) as hidden:
                gate1 = hidden.tile([P, v_passes, NODES, PACK], F32, bufs=1)

                def layer1_silu():
                    for col0 in range(0, HID_S, CHUNK):
                        layer1_weights(col0)
                        for h in range(col0 // K_PASS, (col0 + CHUNK) // K_PASS):
                            s_grouped = hidden.tile([P, NODES, PACK], BF16, align_bytes=64)
                            for nt in range(NODE_TILES):
                                bank = layer1_scalars(h * K_PASS, nt)
                                nc.scalar.activation(
                                    out=s_grouped[:, nt * P : (nt + 1) * P, :],
                                    in_=bank[:].rearrange("p t n -> p n t"),
                                    func=ACT.Silu,
                                    scale=1.0 / math.sqrt(IN_S),
                                )
                            nc.vector.quantize_mx(
                                out=g1s_codes[:, h, :].bitcast(FP8X4),
                                scales=g1s_scales[:, h, :],
                                in_=s_grouped[:].rearrange("p n t -> p (n t)"),
                            )

                def layer1_gates():
                    layer1_weights(HID_S)
                    for h in range(v_passes):
                        for nt in range(NODE_TILES):
                            bank = layer1_scalars(HID_S + h * K_PASS, nt)
                            nc.scalar.activation(
                                out=gate1[:, h, nt * P : (nt + 1) * P, :],
                                in_=bank[:].rearrange("p t n -> p n t"),
                                func=ACT.Tanh,
                                scale=0.5 / math.sqrt(IN_S),
                            )
                        gate_h = gate1[:, h, :, :].rearrange("p n t -> p (n t)")
                        nc.vector.tensor_scalar(
                            out=gate_h,
                            in0=gate_h,
                            scalar1=0.5 / math.sqrt(IN_V),
                            scalar2=0.5 / math.sqrt(IN_V),
                            op0=ALU.mult,
                            op1=ALU.add,
                        )

                def layer1_vectors():
                    def quantise_v(h, d, v_grouped):
                        nc.vector.quantize_mx(
                            out=g1v_codes[:, h, d, :].bitcast(FP8X4),
                            scales=g1v_scales[:, h, d, :],
                            in_=v_grouped[:].rearrange("p n t -> p (n t)"),
                        )

                    waiting = []
                    for h, d in [(h, d) for h in range(v_passes) for d in range(DV)]:
                        v_grouped = hidden.tile([P, NODES, PACK], BF16, align_bytes=64)
                        for nt in range(NODE_TILES):
                            nodes = slice(nt * P, (nt + 1) * P)
                            bank = psum_v.tile([P, PACK, P], F32, tag="bank")
                            for t in range(PACK):
                                chans = slice(h * K_PASS + t * P, h * K_PASS + (t + 1) * P)
                                mx(
                                    bank[:, t, :],
                                    w11_codes[:, chans],
                                    w11_scales[:, chans],
                                    xv_codes[:, d, nodes],
                                    xv_scales[:, d, nodes],
                                    start=True,
                                    stop=True,
                                )
                            nc.vector.tensor_tensor(
                                out=v_grouped[:, nodes, :],
                                in0=bank[:].rearrange("p t n -> p n t"),
                                in1=gate1[:, h, nodes, :],
                                op=ALU.mult,
                            )
                            if nt == 0 and waiting:
                                quantise_v(*waiting.pop())
                        waiting.append((h, d, v_grouped))
                    quantise_v(*waiting.pop())

                layer1_gates()
                layer1_silu()
                layer1_vectors()

        units = []
        begun = []

        def side(n):
            for j in range(n + 1):
                while units and len(begun) < UNIT_LEAD:
                    tensor_part, evacuate = units.pop(0)
                    begun.append((evacuate, tensor_part()))
                if j < n and begun:
                    evacuate, got = begun.pop(0)
                    evacuate(got)

        def layer2_scalars(cols_n, n_side, acts=()):
            acts = list(acts)
            banks = [
                [psum_s.tile([P, BANK], F32, name="acc", tag="bank") for j in range(cols_n // BANK)]
                for nt in range(NODE_TILES)
            ]
            for h in range(s_passes):
                w20_codes = stream.tile([P, CHUNK], U32, bufs=W20_BUFS, align_bytes=64)
                w20_scales = stream.tile([P, CHUNK], U8, bufs=W20_BUFS, align_bytes=64)
                next_weights(w20_codes[:, :cols_n], w20_scales[:, :cols_n])
                if h == 0:
                    for act in acts:
                        act()
                for j in range(cols_n // BANK):
                    cols = slice(j * BANK, (j + 1) * BANK)
                    for nt in range(NODE_TILES):
                        nodes = slice(nt * P, (nt + 1) * P)
                        mx(
                            banks[nt][j][:],
                            g1s_codes[:, h, nodes],
                            g1s_scales[:, h, nodes],
                            w20_codes[:, cols],
                            w20_scales[:, cols],
                            start=(h == 0),
                            stop=(h == s_passes - 1),
                        )
                side(n_side)
            return banks

        compute = {mybir.EngineType.PE, mybir.EngineType.DVE, mybir.EngineType.Activation}
        with tc.tile_pool(name="layer2", bufs=8) as layer2, tc.manual_schedule(engines=compute):
            banks = layer2_scalars(CHUNK, 0)

            def gates2(banks):
                for nt in range(NODE_TILES):
                    for j in range(CHUNK // BANK):
                        nc.scalar.activation(
                            out=gate2[:, nt, j * BANK : (j + 1) * BANK],
                            in_=banks[nt][j][:],
                            func=ACT.Tanh,
                            scale=0.5 / math.sqrt(HID_S),
                        )

            def rescale2():
                for nt in range(NODE_TILES):
                    nc.vector.tensor_scalar(
                        out=gate2[:, nt, :],
                        in0=gate2[:, nt, :],
                        scalar1=0.5 / math.sqrt(HID_V),
                        scalar2=0.5 / math.sqrt(HID_V),
                        op0=ALU.mult,
                        op1=ALU.add,
                    )

            outs = {}

            def out_unit(nt, c):
                nodes = slice(nt * P, (nt + 1) * P)
                chans = slice(c * P, (c + 1) * P)
                per = V_STORE // P

                def tensor_part():
                    bank = psum_v.tile([P, DV, P], F32, tag="bank")
                    for d in range(DV):
                        for h in range(v_passes):
                            mx(
                                bank[:, d, :],
                                g1v_codes[:, h, d, nodes],
                                g1v_scales[:, h, d, nodes],
                                w21_codes[:, h, chans],
                                w21_scales[:, h, chans],
                                start=(h == 0),
                                stop=(h == v_passes - 1),
                            )
                    return bank

                def evacuate(bank):
                    if c % per == 0:
                        v_out = layer2.tile([P, V_STORE, DV], F32, bufs=4)
                        outs[nt, c // per] = v_out
                    v_out = outs[nt, c // per]
                    nc.vector.tensor_tensor(
                        out=v_out[:, (c % per) * P : (c % per + 1) * P, :],
                        in0=bank[:].rearrange("p d o -> p o d"),
                        in1=gate2[:, nt, chans].unsqueeze(2).to_broadcast([P, P, DV]),
                        op=ALU.mult,
                    )
                    if c % per == per - 1:
                        c0 = (c // per) * V_STORE
                        nc.sync.dma_start(
                            out=out[nodes, HID_S + DV * c0 : HID_S + DV * (c0 + V_STORE)],
                            in_=v_out[:].rearrange("p o d -> p (o d)"),
                        )

                return tensor_part, evacuate

            def silu_acts(banks, col0, n):
                return [lambda j=j, nt=nt: silu_out(banks, col0, j, nt) for j in range(n // BANK) for nt in range(NODE_TILES)]

            def silu_out(banks, col0, j, nt):
                s_out = layer2.tile([P, BANK], F32)
                nc.scalar.activation(
                    out=s_out[:],
                    in_=banks[nt][j][:],
                    func=ACT.Silu,
                    scale=1.0 / math.sqrt(HID_S),
                )
                nc.sync.dma_start(
                    out=out[nt * P : (nt + 1) * P, col0 + j * BANK : col0 + (j + 1) * BANK],
                    in_=s_out[:],
                )

            next_weights(w21_codes[:, 0, :], w21_scales[:, 0, :])
            gates2(banks)
            next_weights(w21_codes[:, 1, :], w21_scales[:, 1, :])
            rescale2()
            units.extend([out_unit(nt, c) for nt in range(NODE_TILES) for c in range(HID_V // P)])
            side(0)
            banks = layer2_scalars(CHUNK, UNITS_E)
            acts = silu_acts(banks, 0, CHUNK)
            for j in range(LAST_PARTS):
                banks = layer2_scalars(last, UNITS_F, acts)
                acts = silu_acts(banks, CHUNK + j * last, last)
            for act in acts:
                act()
            side(len(units) + len(begun))
